import numpy as np
import ml_dtypes


def mxq(x, axis, fmt="e4m3"):
    dtype, down = {"e4m3": (ml_dtypes.float8_e4m3fn, 7), "e5m2": (ml_dtypes.float8_e5m2, 14)}[fmt]
    v = np.moveaxis(np.asarray(x, np.float32).astype(ml_dtypes.bfloat16).astype(np.float64), axis, -1)
    blocks = v.reshape(v.shape[:-1] + (-1, 32))
    amax = np.abs(blocks).max(-1, keepdims=True)
    byte = np.maximum(np.where(amax > 0, np.frexp(amax)[1] - 1 + 127, 0) - down, 1)
    scale = np.exp2(byte - 127.0)
    codes = (blocks / scale).astype(np.float32).astype(dtype).astype(np.float64)
    return np.moveaxis((codes * scale).reshape(v.shape), -1, axis)


WIDE = False


def mx_kscale(k):
    if not WIDE:
        return np.ones(k)
    levels = np.array([10, -10, 5, -5, 0])
    if k % 512:
        return np.exp2(np.random.permutation(np.resize(levels, k // 32))).repeat(32)
    a = np.empty((k // 512, 16))
    for p in range(k // 512):
        a[p, :8] = np.random.permutation(np.resize(levels, 8))
        for g in range(8):
            far = levels[np.abs(levels - a[p, g]) >= 10]
            a[p, g + 8] = far[np.random.randint(len(far))]
    return np.exp2(a.ravel()).repeat(32)


BF16 = ml_dtypes.bfloat16


def bf(x):
    return np.asarray(x, np.float32).astype(BF16)


def f64(x):
    return np.asarray(x).astype(np.float64)


B, T, D, H, HD, F = 2, 512, 1024, 16, 64, 4096
A = H * HD
EPS = 1e-5
ERF_H = 0.5
ERF_N = 14


def layernorm(x, g, b):
    mu = np.mean(x, axis=-1, keepdims=True)
    var = np.mean(np.square(x - mu), axis=-1, keepdims=True)
    return (x - mu) / np.sqrt(var + EPS) * g + b


def erf(z):
    acc = np.zeros_like(z)
    for n in range(ERF_N):
        tn = (n + 0.5) * ERF_H
        acc = acc + np.exp(-tn * tn) / (tn * tn + z * z)
    return np.tanh(np.pi * z / ERF_H) - 2.0 * ERF_H * z * np.exp(-z * z) / np.pi * acc


def gelu_erf(v):
    return 0.5 * v * (1.0 + erf(v / np.sqrt(2.0)))


def setup_inputs():
    s, t = mx_kscale(A), mx_kscale(D)
    return {"attn": bf(np.random.standard_normal((B, T, A)) * 0.25 * s),
            "x": bf(np.random.standard_normal((B, T, D)) + 0.5 * np.random.standard_normal((B, T, 1))),
            "w_out": bf(np.random.standard_normal((A, D)) * 2.0 / np.sqrt(A) / s[:, None]),
            "b_out": bf(0.1 * np.random.standard_normal(D)),
            "ln2_g": bf((1.0 + 0.1 * np.random.standard_normal(D)) * t),
            "ln2_b": bf(0.1 * np.random.standard_normal(D) * t),
            "w1": bf(np.random.standard_normal((D, F)) / np.sqrt(D) / t[:, None]),
            "b1": bf(0.2 * np.random.standard_normal(F))}


def reference(attn, x, w_out, b_out, ln2_g, ln2_b, w1, b1):
    x_mid = f64(x) + ((mxq(f64(attn), 2, "e4m3") @ mxq(f64(w_out), 0, "e4m3")) + f64(b_out))
    h2 = layernorm(x_mid, f64(ln2_g), f64(ln2_b))
    hid = gelu_erf((mxq(h2, 2, "e4m3") @ mxq(f64(w1), 0, "e4m3")) + f64(b1))
    return x_mid, hid

@@ -1,0 +1,324 @@
+from contextlib import ExitStack
+
+import concourse.masks as masks
+import concourse.mybir as mybir
+
+F32 = mybir.dt.float32
+BF16 = mybir.dt.bfloat16
+U32 = mybir.dt.uint32
+U8 = mybir.dt.uint8
+FP8X4 = mybir.dt.float8_e4m3fn_x4
+ALU = mybir.AluOpType
+ACT = mybir.ActivationFunctionType
+
+P = 128
+PACK = 4
+K_PASS = P * PACK
+BANK = 512
+RUN = 4
+
+TOKENS = 1024
+WIDTH = 1024
+HIDDEN = 4096
+EPS = 1e-5
+TOKEN_TILES = TOKENS // P
+K_ROWS = WIDTH // P
+PASSES = WIDTH // K_PASS
+CHUNK = 1024
+CHUNKS = HIDDEN // CHUNK
+PIECE = BANK
+PIECES_PER_CHUNK = PASSES * (CHUNK // PIECE)
+W1_PIECES = CHUNKS * PIECES_PER_CHUNK
+VECTOR_EVERY = 4
+FILL = 2
+FIRST_TILES = 2
+
+FLOPS = 2 * TOKENS * WIDTH * WIDTH + 2 * TOKENS * WIDTH * HIDDEN
+
+
+def regroup(copy, grouped, rows):
+    copy(
+        out=grouped.rearrange("p (a i t) -> p a t i", i=RUN, t=PACK),
+        in_=rows.rearrange("p t (a i) -> p a t i", i=RUN),
+    )
+
+
+def tile_transformerblock_pb_kernel(tc, attn, x, w_out, b_out, ln2_g, ln2_b, w1, b1, out_0, out_1):
+    nc = tc.nc
+    attn_rows = attn.flatten_outer_dims().rearrange("(p i) k -> p i k", i=TOKEN_TILES)
+    x_rows = x.flatten_outer_dims().rearrange("(p i) d -> p i d", i=TOKEN_TILES)
+    x_mid_rows = out_0.flatten_outer_dims().rearrange("(p i) d -> p i d", i=TOKEN_TILES)
+    hid_rows = out_1.flatten_outer_dims().rearrange("(p i) f -> p i f", i=TOKEN_TILES)
+    w_out_rows = w_out.rearrange("(g p t) n -> g p t n", g=PASSES, p=P, t=PACK)
+    w1_rows = w1.rearrange("(c p t) f -> c p t f", c=PASSES, p=P, t=PACK)
+
+    with ExitStack() as ctx:
+        keep = ctx.enter_context(tc.tile_pool(name="keep", bufs=1))
+        raw = ctx.enter_context(tc.tile_pool(name="raw", bufs=3))
+        pieces = ctx.enter_context(tc.tile_pool(name="pieces", bufs=3))
+        packs = ctx.enter_context(tc.tile_pool(name="packs", bufs=2))
+        rows = ctx.enter_context(tc.tile_pool(name="rows", bufs=14))
+        psum = ctx.enter_context(tc.psum_pool(name="psum", bufs=8))
+
+        def bank(name):
+            return psum.tile([P, BANK], F32, name=name, tag="bank")
+
+        b_out_row = keep.tile([P, WIDTH], BF16, name="b_out_row")
+        nc.vector.memset(b_out_row[:], 0.0)
+        nc.sync.dma_start(out=b_out_row[0:1, :], in_=b_out.rearrange("(o d) -> o d", o=1))
+        gain_raw = keep.tile([P, PASSES, PACK], BF16, name="gain_raw")
+        bias_raw = keep.tile([P, PASSES, PACK], BF16, name="bias_raw")
+        nc.sync.dma_start(out=gain_raw[:], in_=ln2_g.rearrange("(c p t) -> p c t", c=PASSES, t=PACK))
+        nc.sync.dma_start(out=bias_raw[:], in_=ln2_b.rearrange("(c p t) -> p c t", c=PASSES, t=PACK))
+
+        def raw_tile(name):
+            return raw.tile([P, PASSES * PACK, CHUNK], BF16, name=name, tag="raw")
+
+        def load_w1_chunk(j):
+            w1_raw[j] = raw_tile("w1_raw%d" % j)
+            for c in range(PASSES):
+                nc.sync.dma_start(
+                    out=w1_raw[j][:, PACK * c : PACK * (c + 1), :], in_=w1_rows[c, :, :, CHUNK * j : CHUNK * (j + 1)]
+                )
+
+        w_out_raw = raw_tile("w_out_raw")
+        for g in range(PASSES):
+            nc.sync.dma_start(out=w_out_raw[:, PACK * g : PACK * (g + 1), :], in_=w_out_rows[g])
+        attn_raw = raw_tile("attn_raw")
+        x_raw = keep.tile([P, TOKEN_TILES, WIDTH], BF16, name="x_raw")
+        for tiles in (slice(0, FIRST_TILES), slice(FIRST_TILES, TOKEN_TILES)):
+            nc.sync.dma_start(out=attn_raw[:, tiles, :], in_=attn_rows[:, tiles, :])
+            nc.sync.dma_start(out=x_raw[:, tiles, :], in_=x_rows[:, tiles, :])
+        w1_raw = {}
+        for j in range(CHUNKS - 1):
+            load_w1_chunk(j)
+        b1_all = keep.tile([P, HIDDEN], BF16, name="b1_all")
+        nc.sync.dma_start(out=b1_all[:], in_=b1.partition_broadcast(P))
+
+        neg_half = keep.tile([P, TOKEN_TILES], F32, name="neg_half")
+        nc.vector.memset(neg_half[:], -0.5)
+        table_warm = keep.tile([P, 1], F32, name="table_warm")
+        nc.scalar.activation(out=table_warm[:], in_=neg_half[:, 0:1], func=ACT.Gelu)
+        identity = keep.tile([P, P], F32, name="identity")
+        masks.make_identity(nc, identity[:])
+
+        ones = keep.tile([P, P], BF16, name="ones")
+        nc.vector.memset(ones[:], 1.0)
+        b_out_all = keep.tile([P, WIDTH], BF16, name="b_out_all")
+        for n in range(WIDTH // BANK):
+            cols = slice(BANK * n, BANK * (n + 1))
+            spread = bank("spread")
+            nc.tensor.matmul(out=spread[:], lhsT=ones[:], rhs=b_out_row[:, cols], start=True, stop=True)
+            nc.scalar.copy(out=b_out_all[:, cols], in_=spread[:])
+
+        def quantised(name, outer, width):
+            words = keep.tile([P, outer, width], U32, name=name + "_words", align_bytes=64)
+            scales = keep.tile([P, outer, width], U8, name=name + "_scales", align_bytes=64)
+            return words, scales
+
+        w_out_words, w_out_scales = quantised("w_out", PASSES, WIDTH)
+        w1_words, w1_scales = quantised("w1", PASSES, HIDDEN)
+        attn_words, attn_scales = quantised("attn", TOKEN_TILES, PASSES * P)
+        h2_words, h2_scales = quantised("h2", TOKEN_TILES, PASSES * P)
+
+        def quantise(grouped, words, scales):
+            nc.vector.quantize_mx(out=words.bitcast(FP8X4), scales=scales, in_=grouped)
+
+        def multiply(acc, lhs_words, lhs_scales, i, rhs_words, rhs_scales, cols):
+            for c in range(PASSES):
+                tokens = slice(P * c, P * (c + 1))
+                nc.tensor.matmul_mx(
+                    out=acc,
+                    lhsT=lhs_words[:, i, tokens].bitcast(FP8X4),
+                    lhsT_scale=lhs_scales[:, i, tokens],
+                    rhs=rhs_words[:, c, cols].bitcast(FP8X4),
+                    rhs_scale=rhs_scales[:, c, cols],
+                    start=(c == 0),
+                    stop=(c == PASSES - 1),
+                )
+
+        piece_tiles = {}
+
+        def regroup_piece(key, copy, raw_rows):
+            piece_tiles[key] = pieces.tile([P, PACK * PIECE], BF16, name="piece", tag="piece", align_bytes=64)
+            regroup(copy, piece_tiles[key][:], raw_rows)
+
+        def w1_piece(k):
+            j, rest = divmod(k, PIECES_PER_CHUNK)
+            c, n = divmod(rest, CHUNK // PIECE)
+            return j, c, slice(CHUNK * j + PIECE * n, CHUNK * j + PIECE * (n + 1)), slice(PIECE * n, PIECE * (n + 1))
+
+        def regroup_w1_piece(k, copy):
+            j, c, cols, cols_in_chunk = w1_piece(k)
+            regroup_piece(("w1", k), copy, w1_raw[j][:, PACK * c : PACK * (c + 1), cols_in_chunk])
+
+        def quantise_w1_piece(k):
+            j, c, cols, cols_in_chunk = w1_piece(k)
+            quantise(piece_tiles[("w1", k)][:], w1_words[:, c, cols], w1_scales[:, c, cols])
+
+        def prepare_w1(k):
+            if k < W1_PIECES:
+                regroup_w1_piece(k, nc.vector.tensor_copy if k % VECTOR_EVERY == 0 else nc.scalar.copy)
+            if 1 <= k <= W1_PIECES:
+                quantise_w1_piece(k - 1)
+
+        w_out_pieces = [(g, slice(PIECE * n, PIECE * (n + 1))) for g in range(PASSES) for n in range(WIDTH // PIECE)]
+        for k in range(len(w_out_pieces) + 1):
+            if k < len(w_out_pieces):
+                g, cols = w_out_pieces[k]
+                copy = nc.vector.tensor_copy if k % 2 == 0 else nc.scalar.copy
+                regroup_piece(("w_out", k), copy, w_out_raw[:, PACK * g : PACK * (g + 1), cols])
+            if k > 0:
+                g, cols = w_out_pieces[k - 1]
+                quantise(piece_tiles[("w_out", k - 1)][:], w_out_words[:, g, cols], w_out_scales[:, g, cols])
+
+        attn_grouped = {}
+
+        def transpose_attn(i):
+            attn_pairs = attn_raw[:, i, :].bitcast(F32)
+            attn_t = bank("attn_t")
+            for g in range(PASSES):
+                for u in range(2):
+                    nc.tensor.transpose(
+                        out=attn_t[:, PASSES * P * u + P * g : PASSES * P * u + P * (g + 1)],
+                        in_=attn_pairs[:, 2 * P * g + u : 2 * P * (g + 1) : 2],
+                        identity=identity[:],
+                    )
+            attn_grouped[i] = packs.tile([P, PACK * PASSES * P], BF16, name="attn_grouped", align_bytes=64)
+            nc.scalar.copy(
+                out=attn_grouped[i][:].bitcast(F32).rearrange("q (m u) -> q m u", u=2),
+                in_=attn_t[:].rearrange("q (u m) -> q m u", u=2),
+            )
+
+        def quantise_attn(i):
+            quantise(attn_grouped[i][:], attn_words[:, i, :], attn_scales[:, i, :])
+
+        for i in range(FIRST_TILES):
+            transpose_attn(i)
+        for i in range(FIRST_TILES):
+            quantise_attn(i)
+
+        gain_bias = keep.tile([P, 2 * K_ROWS], F32, name="gain_bias")
+        nc.vector.tensor_copy(out=gain_bias[:, 0:K_ROWS], in_=gain_raw[:].rearrange("p c t -> p (c t)"))
+        nc.vector.tensor_copy(out=gain_bias[:, K_ROWS:], in_=bias_raw[:].rearrange("p c t -> p (c t)"))
+
+        def row(name):
+            return rows.tile([P, WIDTH], F32, name=name, tag="row")
+
+        x_mid = {}
+        row_sums = keep.tile([P, TOKEN_TILES, WIDTH // BANK], F32, name="row_sums")
+        scaled_sums = keep.tile([P, WIDTH // BANK], F32, name="scaled_sums")
+        neg_mean = keep.tile([P, TOKEN_TILES], F32, name="neg_mean")
+        squares = keep.tile([P, WIDTH], BF16, name="squares")
+        sum_sq = keep.tile([P, TOKEN_TILES], F32, name="sum_sq")
+
+        def project(i):
+            x_bias = row("x_bias")
+            nc.vector.tensor_tensor(out=x_bias[:], in0=x_raw[:, i, :], in1=b_out_all[:], op=ALU.add)
+            x_mid[i] = row("x_mid")
+            for n in range(WIDTH // BANK):
+                cols = slice(BANK * n, BANK * (n + 1))
+                acc = bank("acc1")
+                multiply(acc[:], attn_words, attn_scales, i, w_out_words, w_out_scales, cols)
+                nc.vector.scalar_tensor_tensor(
+                    out=x_mid[i][:, cols], in0=acc[:], scalar=1.0, in1=x_bias[:, cols],
+                    op0=ALU.mult, op1=ALU.add, accum_out=row_sums[:, i, n : n + 1],
+                )
+            nc.sync.dma_start(out=x_mid_rows[:, i, :], in_=x_mid[i][:])
+            nc.scalar.activation(
+                out=scaled_sums[:], in_=row_sums[:, i, :], func=ACT.Identity, scale=-1.0 / WIDTH,
+                accum_out=neg_mean[:, i : i + 1],
+            )
+            nc.scalar.activation(
+                out=squares[:], in_=x_mid[i][:], func=ACT.Square, bias=neg_mean[:, i : i + 1],
+                accum_out=sum_sq[:, i : i + 1],
+            )
+
+        for i in range(TOKEN_TILES):
+            project(i)
+            if i % 2 == 0 and i + 2 < TOKEN_TILES:
+                transpose_attn(i + 2)
+                transpose_attn(i + 3)
+            if i % 2 == 1 and i + 1 < TOKEN_TILES:
+                quantise_attn(i + 1)
+                quantise_attn(i + 2)
+            if i >= TOKEN_TILES - PIECES_PER_CHUNK:
+                prepare_w1(i - (TOKEN_TILES - PIECES_PER_CHUNK))
+        load_w1_chunk(CHUNKS - 1)
+
+        var_eps = keep.tile([P, TOKEN_TILES], F32, name="var_eps")
+        nc.gpsimd.tensor_scalar(out=var_eps[:], in0=sum_sq[:], scalar1=1.0 / WIDTH, scalar2=EPS, op0=ALU.mult, op1=ALU.add)
+        rstd = keep.tile([P, TOKEN_TILES], F32, name="rstd")
+        nc.gpsimd.tensor_tensor(out=rstd[:], in0=var_eps[:], in1=neg_half[:], op=ALU.pow)
+        for k in range(PIECES_PER_CHUNK, PIECES_PER_CHUNK + FILL):
+            prepare_w1(k)
+
+        h2_planes = {}
+        h2_grouped = {}
+        hid_acc = {}
+
+        def normalise_and_transpose(i):
+            normed = row("normed")
+            nc.vector.tensor_scalar(
+                out=normed[:].rearrange("n (c t p) -> n c t p", c=PASSES, t=PACK),
+                in0=x_mid[i][:].rearrange("n (c p t) -> n c t p", c=PASSES, t=PACK), scalar1=neg_mean[:, i : i + 1], scalar2=rstd[:, i : i + 1],
+                op0=ALU.add, op1=ALU.mult,
+            )
+            normed_t = [bank("normed_t%d" % c) for c in range(PASSES)]
+            for r in range(K_ROWS):
+                c, t = divmod(r, PACK)
+                nc.tensor.transpose(
+                    out=normed_t[c][:, P * t : P * (t + 1)], in_=normed[:, P * r : P * (r + 1)], identity=identity[:]
+                )
+            h2_planes[i] = packs.tile([P, PACK, PASSES * P], BF16, name="h2_planes")
+            for r in range(K_ROWS):
+                c, t = divmod(r, PACK)
+                nc.scalar.activation(
+                    out=h2_planes[i][:, t, P * c : P * (c + 1)], in_=normed_t[c][:, P * t : P * (t + 1)],
+                    func=ACT.Identity, scale=gain_bias[:, r : r + 1], bias=gain_bias[:, K_ROWS + r : K_ROWS + r + 1],
+                )
+
+        def regroup_h2(i):
+            h2_grouped[i] = packs.tile([P, PACK * PASSES * P], BF16, name="h2_grouped", align_bytes=64)
+            regroup(nc.vector.tensor_copy, h2_grouped[i][:], h2_planes[i][:])
+
+        def quantise_h2(i):
+            quantise(h2_grouped[i][:], h2_words[:, i, :], h2_scales[:, i, :])
+
+        def hid_matmul(j, i):
+            hid_acc[(j, i)] = [bank("acc2_%d" % n) for n in range(CHUNK // BANK)]
+            for n in range(CHUNK // BANK):
+                cols = slice(CHUNK * j + BANK * n, CHUNK * j + BANK * (n + 1))
+                multiply(hid_acc[(j, i)][n][:], h2_words, h2_scales, i, w1_words, w1_scales, cols)
+
+        def hid_finish(j, i, banks_at_a_time):
+            hid = row("hid")
+            for first in range(0, CHUNK // BANK, banks_at_a_time):
+                for n in range(first, first + banks_at_a_time):
+                    nc.vector.tensor_tensor(
+                        out=hid[:, BANK * n : BANK * (n + 1)], in0=hid_acc[(j, i)][n][:],
+                        in1=b1_all[:, CHUNK * j + BANK * n : CHUNK * j + BANK * (n + 1)], op=ALU.add,
+                    )
+                part = slice(BANK * first, BANK * (first + banks_at_a_time))
+                nc.scalar.activation(out=hid[:, part], in_=hid[:, part], func=ACT.Gelu)
+                nc.sync.dma_start(
+                    out=hid_rows[:, i, CHUNK * j + BANK * first : CHUNK * j + BANK * (first + banks_at_a_time)],
+                    in_=hid[:, part],
+                )
+
+        for r in range(TOKEN_TILES + 3):
+            if r < TOKEN_TILES:
+                normalise_and_transpose(r)
+            if 2 <= r < TOKEN_TILES + 2:
+                regroup_h2(r - 2)
+            prepare_w1(PIECES_PER_CHUNK + FILL + r)
+            if 2 <= r < TOKEN_TILES + 2:
+                quantise_h2(r - 2)
+                hid_matmul(0, r - 2)
+            if r >= 3:
+                hid_finish(0, r - 3, CHUNK // BANK)
+        for j in range(1, CHUNKS):
+            for i in range(TOKEN_TILES):
+                last = j == CHUNKS - 1 and i == TOKEN_TILES - 1
+                hid_matmul(j, i)
+                hid_finish(j, i, 1 if last else CHUNK // BANK)

@@ -101,6 +101,8 @@ def tile_transformerblock_pb_kernel(tc, attn, x, w_out, b_out, ln2_g, ln2_b, w1,
         nc.scalar.activation(out=table_warm[:], in_=neg_half[:, 0:1], func=ACT.Gelu)
         identity = keep.tile([P, P], F32, name="identity")
         masks.make_identity(nc, identity[:])
+        identity_bf16 = keep.tile([P, P], BF16, name="identity_bf16")
+        nc.vector.tensor_copy(out=identity_bf16[:], in_=identity[:])
 
         ones = keep.tile([P, P], BF16, name="ones")
         nc.vector.memset(ones[:], 1.0)
@@ -152,13 +154,32 @@ def tile_transformerblock_pb_kernel(tc, attn, x, w_out, b_out, ln2_g, ln2_b, w1,
             j, c, cols, cols_in_chunk = w1_piece(k)
             regroup_piece(("w1", k), copy, w1_raw[j][:, PACK * c : PACK * (c + 1), cols_in_chunk])
 
+        def regroup_w1_by_matmul(k):
+            j, c, cols, cols_in_chunk = w1_piece(k)
+            grouped = pieces.tile([P, PACK * PIECE], BF16, name="piece", tag="piece", align_bytes=64)
+            piece_tiles[("w1", k)] = grouped
+            width = BANK // PACK
+            for half in range(2):
+                regrouped = psum.tile([P, 2 * BANK], BF16, name="regrouped", tag="bank")
+                for n in range(2):
+                    first = cols_in_chunk.start + width * (2 * half + n)
+                    nc.tensor.matmul(
+                        out=regrouped[:, BANK * n : BANK * (n + 1)], lhsT=identity_bf16[:],
+                        rhs=w1_raw[j][:, PACK * c : PACK * (c + 1), first : first + width].rearrange("p t w -> p w t"),
+                        start=True, stop=True,
+                    )
+                nc.scalar.copy(out=grouped[:, 2 * BANK * half : 2 * BANK * (half + 1)], in_=regrouped[:])
+
         def quantise_w1_piece(k):
             j, c, cols, cols_in_chunk = w1_piece(k)
             quantise(piece_tiles[("w1", k)][:], w1_words[:, c, cols], w1_scales[:, c, cols])
 
         def prepare_w1(k):
             if k < W1_PIECES:
-                regroup_w1_piece(k, nc.vector.tensor_copy if k % VECTOR_EVERY == 0 else nc.scalar.copy)
+                if k % VECTOR_EVERY == 0:
+                    regroup_w1_piece(k, nc.vector.tensor_copy)
+                else:
+                    regroup_w1_by_matmul(k)
             if 1 <= k <= W1_PIECES:
                 quantise_w1_piece(k - 1)
 

@@ -15,6 +15,7 @@ P = 128
 PACK = 4
 K_PASS = P * PACK
 BANK = 512
+RUN_K = 8
 RUN = 4
 
 TOKENS = 1024
@@ -29,7 +30,6 @@ CHUNKS = HIDDEN // CHUNK
 PIECE = BANK
 PIECES_PER_CHUNK = PASSES * (CHUNK // PIECE)
 W1_PIECES = CHUNKS * PIECES_PER_CHUNK
-VECTOR_EVERY = 4
 FILL = 2
 FIRST_TILES = 2
 
@@ -50,7 +50,7 @@ def tile_transformerblock_pb_kernel(tc, attn, x, w_out, b_out, ln2_g, ln2_b, w1,
     x_mid_rows = out_0.flatten_outer_dims().rearrange("(p i) d -> p i d", i=TOKEN_TILES)
     hid_rows = out_1.flatten_outer_dims().rearrange("(p i) f -> p i f", i=TOKEN_TILES)
     w_out_rows = w_out.rearrange("(g p t) n -> g p t n", g=PASSES, p=P, t=PACK)
-    w1_rows = w1.rearrange("(c p t) f -> c p t f", c=PASSES, p=P, t=PACK)
+    w1_rows = w1.rearrange("(c b t i) f -> c t b i f", c=PASSES, t=PACK, i=RUN_K)
 
     with ExitStack() as ctx:
         keep = ctx.enter_context(tc.tile_pool(name="keep", bufs=1))
@@ -66,10 +66,15 @@ def tile_transformerblock_pb_kernel(tc, attn, x, w_out, b_out, ln2_g, ln2_b, w1,
         b_out_row = keep.tile([P, WIDTH], BF16, name="b_out_row")
         nc.vector.memset(b_out_row[:], 0.0)
         nc.sync.dma_start(out=b_out_row[0:1, :], in_=b_out.rearrange("(o d) -> o d", o=1))
-        gain_raw = keep.tile([P, PASSES, PACK], BF16, name="gain_raw")
-        bias_raw = keep.tile([P, PASSES, PACK], BF16, name="bias_raw")
-        nc.sync.dma_start(out=gain_raw[:], in_=ln2_g.rearrange("(c p t) -> p c t", c=PASSES, t=PACK))
-        nc.sync.dma_start(out=bias_raw[:], in_=ln2_b.rearrange("(c p t) -> p c t", c=PASSES, t=PACK))
+        gain_bias_rows = keep.tile([P, P], BF16, name="gain_bias_rows")
+        nc.vector.memset(gain_bias_rows[:], 0.0)
+        for v, vector in enumerate((ln2_g, ln2_b)):
+            vector_rows = vector.rearrange("(c b t i) -> c t b i", c=PASSES, t=PACK, i=RUN_K)
+            for c in range(PASSES):
+                first = K_ROWS * v + PACK * c
+                nc.sync.dma_start(
+                    out=gain_bias_rows[first : first + PACK, :].rearrange("t (b i) -> t b i", i=RUN_K), in_=vector_rows[c]
+                )
 
         def raw_tile(name):
             return raw.tile([P, PASSES * PACK, CHUNK], BF16, name=name, tag="raw")
@@ -77,9 +82,10 @@ def tile_transformerblock_pb_kernel(tc, attn, x, w_out, b_out, ln2_g, ln2_b, w1,
         def load_w1_chunk(j):
             w1_raw[j] = raw_tile("w1_raw%d" % j)
             for c in range(PASSES):
-                nc.sync.dma_start(
-                    out=w1_raw[j][:, PACK * c : PACK * (c + 1), :], in_=w1_rows[c, :, :, CHUNK * j : CHUNK * (j + 1)]
-                )
+                for t in range(PACK):
+                    nc.sync.dma_start(
+                        out=w1_raw[j][:, PACK * c + t, :], in_=w1_rows[c, t, :, :, CHUNK * j : CHUNK * (j + 1)]
+                    )
 
         w_out_raw = raw_tile("w_out_raw")
         for g in range(PASSES):
@@ -176,7 +182,7 @@ def tile_transformerblock_pb_kernel(tc, attn, x, w_out, b_out, ln2_g, ln2_b, w1,
 
         def prepare_w1(k):
             if k < W1_PIECES:
-                if k % VECTOR_EVERY == 0:
+                if k == 0:
                     regroup_w1_piece(k, nc.vector.tensor_copy)
                 else:
                     regroup_w1_by_matmul(k)
@@ -219,9 +225,12 @@ def tile_transformerblock_pb_kernel(tc, attn, x, w_out, b_out, ln2_g, ln2_b, w1,
         for i in range(FIRST_TILES):
             quantise_attn(i)
 
+        gain_bias_f32 = keep.tile([P, P], F32, name="gain_bias_f32")
+        nc.vector.tensor_copy(out=gain_bias_f32[:], in_=gain_bias_rows[:])
+        gain_bias_t = bank("gain_bias_t")
+        nc.tensor.transpose(out=gain_bias_t[:, 0:P], in_=gain_bias_f32[:], identity=identity[:])
         gain_bias = keep.tile([P, 2 * K_ROWS], F32, name="gain_bias")
-        nc.vector.tensor_copy(out=gain_bias[:, 0:K_ROWS], in_=gain_raw[:].rearrange("p c t -> p (c t)"))
-        nc.vector.tensor_copy(out=gain_bias[:, K_ROWS:], in_=bias_raw[:].rearrange("p c t -> p (c t)"))
+        nc.vector.tensor_copy(out=gain_bias[:], in_=gain_bias_t[:, 0 : 2 * K_ROWS])
 
         def row(name):
             return rows.tile([P, WIDTH], F32, name=name, tag="row")
@@ -280,9 +289,11 @@ def tile_transformerblock_pb_kernel(tc, attn, x, w_out, b_out, ln2_g, ln2_b, w1,
 
         def normalise_and_transpose(i):
             normed = row("normed")
-            nc.vector.tensor_scalar(
-                out=normed[:].rearrange("n (c t p) -> n c t p", c=PASSES, t=PACK),
-                in0=x_mid[i][:].rearrange("n (c p t) -> n c t p", c=PASSES, t=PACK), scalar1=neg_mean[:, i : i + 1], scalar2=rstd[:, i : i + 1],
+            for c in range(PASSES):
+              cols = slice(K_PASS * c, K_PASS * (c + 1))
+              nc.vector.tensor_scalar(
+                out=normed[:, cols].rearrange("n (t b i) -> n t b i", t=PACK, i=RUN_K),
+                in0=x_mid[i][:, cols].rearrange("n (b t i) -> n t b i", t=PACK, i=RUN_K), scalar1=neg_mean[:, i : i + 1], scalar2=rstd[:, i : i + 1],
                 op0=ALU.add, op1=ALU.mult,
             )
             normed_t = [bank("normed_t%d" % c) for c in range(PASSES)]

@@ -15,6 +15,8 @@ P = 128
 PACK = 4
 K_PASS = P * PACK
 BANK = 512
+RAW_BUFS = 3
+SCALAR_PIECES = (3, 5, 7, 9, 11)
 RUN_K = 8
 RUN = 4
 
@@ -30,8 +32,9 @@ CHUNKS = HIDDEN // CHUNK
 PIECE = BANK
 PIECES_PER_CHUNK = PASSES * (CHUNK // PIECE)
 W1_PIECES = CHUNKS * PIECES_PER_CHUNK
-FILL = 2
-FIRST_TILES = 2
+PAIR = 2
+PAIRS = TOKEN_TILES // PAIR
+PAIR_TOKENS = PAIR * P
 
 FLOPS = 2 * TOKENS * WIDTH * WIDTH + 2 * TOKENS * WIDTH * HIDDEN
 
@@ -54,10 +57,10 @@ def tile_transformerblock_pb_kernel(tc, attn, x, w_out, b_out, ln2_g, ln2_b, w1,
 
     with ExitStack() as ctx:
         keep = ctx.enter_context(tc.tile_pool(name="keep", bufs=1))
-        raw = ctx.enter_context(tc.tile_pool(name="raw", bufs=3))
+        raw = ctx.enter_context(tc.tile_pool(name="raw", bufs=RAW_BUFS))
         pieces = ctx.enter_context(tc.tile_pool(name="pieces", bufs=3))
         packs = ctx.enter_context(tc.tile_pool(name="packs", bufs=2))
-        rows = ctx.enter_context(tc.tile_pool(name="rows", bufs=14))
+        rows = ctx.enter_context(tc.tile_pool(name="rows", bufs=13))
         psum = ctx.enter_context(tc.psum_pool(name="psum", bufs=8))
 
         def bank(name):
@@ -66,18 +69,11 @@ def tile_transformerblock_pb_kernel(tc, attn, x, w_out, b_out, ln2_g, ln2_b, w1,
         b_out_row = keep.tile([P, WIDTH], BF16, name="b_out_row")
         nc.vector.memset(b_out_row[:], 0.0)
         nc.sync.dma_start(out=b_out_row[0:1, :], in_=b_out.rearrange("(o d) -> o d", o=1))
-        gain_bias_rows = keep.tile([P, P], BF16, name="gain_bias_rows")
-        nc.vector.memset(gain_bias_rows[:], 0.0)
-        for v, vector in enumerate((ln2_g, ln2_b)):
-            vector_rows = vector.rearrange("(c b t i) -> c t b i", c=PASSES, t=PACK, i=RUN_K)
-            for c in range(PASSES):
-                first = K_ROWS * v + PACK * c
-                nc.sync.dma_start(
-                    out=gain_bias_rows[first : first + PACK, :].rearrange("t (b i) -> t b i", i=RUN_K), in_=vector_rows[c]
-                )
 
         def raw_tile(name):
             return raw.tile([P, PASSES * PACK, CHUNK], BF16, name=name, tag="raw")
+
+        w1_raw = {}
 
         def load_w1_chunk(j):
             w1_raw[j] = raw_tile("w1_raw%d" % j)
@@ -92,16 +88,24 @@ def tile_transformerblock_pb_kernel(tc, attn, x, w_out, b_out, ln2_g, ln2_b, w1,
             nc.sync.dma_start(out=w_out_raw[:, PACK * g : PACK * (g + 1), :], in_=w_out_rows[g])
         attn_raw = raw_tile("attn_raw")
         x_raw = keep.tile([P, TOKEN_TILES, WIDTH], BF16, name="x_raw")
-        for tiles in (slice(0, FIRST_TILES), slice(FIRST_TILES, TOKEN_TILES)):
+        for tiles in (slice(0, PAIR), slice(PAIR, TOKEN_TILES)):
             nc.sync.dma_start(out=attn_raw[:, tiles, :], in_=attn_rows[:, tiles, :])
             nc.sync.dma_start(out=x_raw[:, tiles, :], in_=x_rows[:, tiles, :])
-        w1_raw = {}
-        for j in range(CHUNKS - 1):
-            load_w1_chunk(j)
+        gain_bias_rows = keep.tile([P, P], BF16, name="gain_bias_rows")
+        nc.vector.memset(gain_bias_rows[:], 0.0)
+        for v, vector in enumerate((ln2_g, ln2_b)):
+            vector_rows = vector.rearrange("(c b t i) -> c t b i", c=PASSES, t=PACK, i=RUN_K)
+            for c in range(PASSES):
+                first = K_ROWS * v + PACK * c
+                nc.sync.dma_start(
+                    out=gain_bias_rows[first : first + PACK, :].rearrange("t (b i) -> t b i", i=RUN_K), in_=vector_rows[c]
+                )
+        load_w1_chunk(0)
+        load_w1_chunk(1)
         b1_all = keep.tile([P, HIDDEN], BF16, name="b1_all")
         nc.sync.dma_start(out=b1_all[:], in_=b1.partition_broadcast(P))
 
-        neg_half = keep.tile([P, TOKEN_TILES], F32, name="neg_half")
+        neg_half = keep.tile([P, PAIR], F32, name="neg_half")
         nc.vector.memset(neg_half[:], -0.5)
         table_warm = keep.tile([P, 1], F32, name="table_warm")
         nc.scalar.activation(out=table_warm[:], in_=neg_half[:, 0:1], func=ACT.Gelu)
@@ -109,15 +113,8 @@ def tile_transformerblock_pb_kernel(tc, attn, x, w_out, b_out, ln2_g, ln2_b, w1,
         masks.make_identity(nc, identity[:])
         identity_bf16 = keep.tile([P, P], BF16, name="identity_bf16")
         nc.vector.tensor_copy(out=identity_bf16[:], in_=identity[:])
-
         ones = keep.tile([P, P], BF16, name="ones")
         nc.vector.memset(ones[:], 1.0)
-        b_out_all = keep.tile([P, WIDTH], BF16, name="b_out_all")
-        for n in range(WIDTH // BANK):
-            cols = slice(BANK * n, BANK * (n + 1))
-            spread = bank("spread")
-            nc.tensor.matmul(out=spread[:], lhsT=ones[:], rhs=b_out_row[:, cols], start=True, stop=True)
-            nc.scalar.copy(out=b_out_all[:, cols], in_=spread[:])
 
         def quantised(name, outer, width):
             words = keep.tile([P, outer, width], U32, name=name + "_words", align_bytes=64)
@@ -127,22 +124,18 @@ def tile_transformerblock_pb_kernel(tc, attn, x, w_out, b_out, ln2_g, ln2_b, w1,
         w_out_words, w_out_scales = quantised("w_out", PASSES, WIDTH)
         w1_words, w1_scales = quantised("w1", PASSES, HIDDEN)
         attn_words, attn_scales = quantised("attn", TOKEN_TILES, PASSES * P)
-        h2_words, h2_scales = quantised("h2", TOKEN_TILES, PASSES * P)
+        h2_words, h2_scales = quantised("h2", PAIRS, PASSES * PAIR_TOKENS)
 
         def quantise(grouped, words, scales):
             nc.vector.quantize_mx(out=words.bitcast(FP8X4), scales=scales, in_=grouped)
 
-        def multiply(acc, lhs_words, lhs_scales, i, rhs_words, rhs_scales, cols):
+        def multiply(acc, words_of_pass, rhs_words, rhs_scales, cols):
             for c in range(PASSES):
-                tokens = slice(P * c, P * (c + 1))
+                lhs_words, lhs_scales = words_of_pass(c)
                 nc.tensor.matmul_mx(
-                    out=acc,
-                    lhsT=lhs_words[:, i, tokens].bitcast(FP8X4),
-                    lhsT_scale=lhs_scales[:, i, tokens],
-                    rhs=rhs_words[:, c, cols].bitcast(FP8X4),
-                    rhs_scale=rhs_scales[:, c, cols],
-                    start=(c == 0),
-                    stop=(c == PASSES - 1),
+                    out=acc, lhsT=lhs_words.bitcast(FP8X4), lhsT_scale=lhs_scales,
+                    rhs=rhs_words[:, c, cols].bitcast(FP8X4), rhs_scale=rhs_scales[:, c, cols],
+                    start=(c == 0), stop=(c == PASSES - 1),
                 )
 
         piece_tiles = {}
@@ -156,38 +149,14 @@ def tile_transformerblock_pb_kernel(tc, attn, x, w_out, b_out, ln2_g, ln2_b, w1,
             c, n = divmod(rest, CHUNK // PIECE)
             return j, c, slice(CHUNK * j + PIECE * n, CHUNK * j + PIECE * (n + 1)), slice(PIECE * n, PIECE * (n + 1))
 
-        def regroup_w1_piece(k, copy):
-            j, c, cols, cols_in_chunk = w1_piece(k)
-            regroup_piece(("w1", k), copy, w1_raw[j][:, PACK * c : PACK * (c + 1), cols_in_chunk])
-
-        def regroup_w1_by_matmul(k):
-            j, c, cols, cols_in_chunk = w1_piece(k)
-            grouped = pieces.tile([P, PACK * PIECE], BF16, name="piece", tag="piece", align_bytes=64)
-            piece_tiles[("w1", k)] = grouped
-            width = BANK // PACK
-            for half in range(2):
-                regrouped = psum.tile([P, 2 * BANK], BF16, name="regrouped", tag="bank")
-                for n in range(2):
-                    first = cols_in_chunk.start + width * (2 * half + n)
-                    nc.tensor.matmul(
-                        out=regrouped[:, BANK * n : BANK * (n + 1)], lhsT=identity_bf16[:],
-                        rhs=w1_raw[j][:, PACK * c : PACK * (c + 1), first : first + width].rearrange("p t w -> p w t"),
-                        start=True, stop=True,
-                    )
-                nc.scalar.copy(out=grouped[:, 2 * BANK * half : 2 * BANK * (half + 1)], in_=regrouped[:])
-
-        def quantise_w1_piece(k):
-            j, c, cols, cols_in_chunk = w1_piece(k)
-            quantise(piece_tiles[("w1", k)][:], w1_words[:, c, cols], w1_scales[:, c, cols])
-
         def prepare_w1(k):
             if k < W1_PIECES:
-                if k == 0:
-                    regroup_w1_piece(k, nc.vector.tensor_copy)
-                else:
-                    regroup_w1_by_matmul(k)
+                j, c, cols, cols_in_chunk = w1_piece(k)
+                copy = nc.scalar.copy if k in SCALAR_PIECES else nc.vector.tensor_copy
+                regroup_piece(("w1", k), copy, w1_raw[j][:, PACK * c : PACK * (c + 1), cols_in_chunk])
             if 1 <= k <= W1_PIECES:
-                quantise_w1_piece(k - 1)
+                j, c, cols, cols_in_chunk = w1_piece(k - 1)
+                quantise(piece_tiles[("w1", k - 1)][:], w1_words[:, c, cols], w1_scales[:, c, cols])
 
         w_out_pieces = [(g, slice(PIECE * n, PIECE * (n + 1))) for g in range(PASSES) for n in range(WIDTH // PIECE)]
         for k in range(len(w_out_pieces) + 1):
@@ -220,38 +189,40 @@ def tile_transformerblock_pb_kernel(tc, attn, x, w_out, b_out, ln2_g, ln2_b, w1,
         def quantise_attn(i):
             quantise(attn_grouped[i][:], attn_words[:, i, :], attn_scales[:, i, :])
 
-        for i in range(FIRST_TILES):
-            transpose_attn(i)
-        for i in range(FIRST_TILES):
-            quantise_attn(i)
-
-        gain_bias_f32 = keep.tile([P, P], F32, name="gain_bias_f32")
-        nc.vector.tensor_copy(out=gain_bias_f32[:], in_=gain_bias_rows[:])
-        gain_bias_t = bank("gain_bias_t")
-        nc.tensor.transpose(out=gain_bias_t[:, 0:P], in_=gain_bias_f32[:], identity=identity[:])
-        gain_bias = keep.tile([P, 2 * K_ROWS], F32, name="gain_bias")
-        nc.vector.tensor_copy(out=gain_bias[:], in_=gain_bias_t[:, 0 : 2 * K_ROWS])
-
         def row(name):
             return rows.tile([P, WIDTH], F32, name=name, tag="row")
 
+        x_bias = {}
         x_mid = {}
         row_sums = keep.tile([P, TOKEN_TILES, WIDTH // BANK], F32, name="row_sums")
         scaled_sums = keep.tile([P, WIDTH // BANK], F32, name="scaled_sums")
         neg_mean = keep.tile([P, TOKEN_TILES], F32, name="neg_mean")
         squares = keep.tile([P, WIDTH], BF16, name="squares")
         sum_sq = keep.tile([P, TOKEN_TILES], F32, name="sum_sq")
+        var_eps = keep.tile([P, TOKEN_TILES], F32, name="var_eps")
+        rstd = keep.tile([P, TOKEN_TILES], F32, name="rstd")
+
+        def add_b_out(i):
+            x_bias[i] = row("x_bias")
+            for n in range(WIDTH // BANK):
+                cols = slice(BANK * n, BANK * (n + 1))
+                sums = bank("x_bias_sums")
+                nc.tensor.matmul(out=sums[:], lhsT=identity_bf16[:], rhs=x_raw[:, i, cols], start=True, stop=False)
+                nc.tensor.matmul(out=sums[:], lhsT=ones[:], rhs=b_out_row[:, cols], start=False, stop=True)
+                nc.scalar.copy(out=x_bias[i][:, cols], in_=sums[:])
 
         def project(i):
-            x_bias = row("x_bias")
-            nc.vector.tensor_tensor(out=x_bias[:], in0=x_raw[:, i, :], in1=b_out_all[:], op=ALU.add)
+            def words_of_pass(c):
+                tokens = slice(P * c, P * (c + 1))
+                return attn_words[:, i, tokens], attn_scales[:, i, tokens]
+
             x_mid[i] = row("x_mid")
             for n in range(WIDTH // BANK):
                 cols = slice(BANK * n, BANK * (n + 1))
                 acc = bank("acc1")
-                multiply(acc[:], attn_words, attn_scales, i, w_out_words, w_out_scales, cols)
+                multiply(acc[:], words_of_pass, w_out_words, w_out_scales, cols)
                 nc.vector.scalar_tensor_tensor(
-                    out=x_mid[i][:, cols], in0=acc[:], scalar=1.0, in1=x_bias[:, cols],
+                    out=x_mid[i][:, cols], in0=acc[:], scalar=1.0, in1=x_bias[i][:, cols],
                     op0=ALU.mult, op1=ALU.add, accum_out=row_sums[:, i, n : n + 1],
                 )
             nc.sync.dma_start(out=x_mid_rows[:, i, :], in_=x_mid[i][:])
@@ -264,72 +235,78 @@ def tile_transformerblock_pb_kernel(tc, attn, x, w_out, b_out, ln2_g, ln2_b, w1,
                 accum_out=sum_sq[:, i : i + 1],
             )
 
-        for i in range(TOKEN_TILES):
-            project(i)
-            if i % 2 == 0 and i + 2 < TOKEN_TILES:
-                transpose_attn(i + 2)
-                transpose_attn(i + 3)
-            if i % 2 == 1 and i + 1 < TOKEN_TILES:
-                quantise_attn(i + 1)
-                quantise_attn(i + 2)
-            if i >= TOKEN_TILES - PIECES_PER_CHUNK:
-                prepare_w1(i - (TOKEN_TILES - PIECES_PER_CHUNK))
-        load_w1_chunk(CHUNKS - 1)
+        def rstd_of_pair(q):
+            tiles = slice(PAIR * q, PAIR * (q + 1))
+            nc.gpsimd.tensor_scalar(
+                out=var_eps[:, tiles], in0=sum_sq[:, tiles], scalar1=1.0 / WIDTH, scalar2=EPS, op0=ALU.mult, op1=ALU.add
+            )
+            nc.gpsimd.tensor_tensor(out=rstd[:, tiles], in0=var_eps[:, tiles], in1=neg_half[:], op=ALU.pow)
 
-        var_eps = keep.tile([P, TOKEN_TILES], F32, name="var_eps")
-        nc.gpsimd.tensor_scalar(out=var_eps[:], in0=sum_sq[:], scalar1=1.0 / WIDTH, scalar2=EPS, op0=ALU.mult, op1=ALU.add)
-        rstd = keep.tile([P, TOKEN_TILES], F32, name="rstd")
-        nc.gpsimd.tensor_tensor(out=rstd[:], in0=var_eps[:], in1=neg_half[:], op=ALU.pow)
-        for k in range(PIECES_PER_CHUNK, PIECES_PER_CHUNK + FILL):
-            prepare_w1(k)
+        gain_bias = keep.tile([P, 2 * K_ROWS], F32, name="gain_bias")
+
+        def prepare_gain_bias():
+            gain_bias_f32 = keep.tile([P, P], F32, name="gain_bias_f32")
+            nc.vector.tensor_copy(out=gain_bias_f32[:], in_=gain_bias_rows[:])
+            gain_bias_t = bank("gain_bias_t")
+            nc.tensor.transpose(out=gain_bias_t[:, 0:P], in_=gain_bias_f32[:], identity=identity[:])
+            nc.vector.tensor_copy(out=gain_bias[:], in_=gain_bias_t[:, 0 : 2 * K_ROWS])
 
         h2_planes = {}
         h2_grouped = {}
-        hid_acc = {}
 
-        def normalise_and_transpose(i):
-            normed = row("normed")
-            for c in range(PASSES):
-              cols = slice(K_PASS * c, K_PASS * (c + 1))
-              nc.vector.tensor_scalar(
-                out=normed[:, cols].rearrange("n (t b i) -> n t b i", t=PACK, i=RUN_K),
-                in0=x_mid[i][:, cols].rearrange("n (b t i) -> n t b i", t=PACK, i=RUN_K), scalar1=neg_mean[:, i : i + 1], scalar2=rstd[:, i : i + 1],
-                op0=ALU.add, op1=ALU.mult,
-            )
-            normed_t = [bank("normed_t%d" % c) for c in range(PASSES)]
-            for r in range(K_ROWS):
-                c, t = divmod(r, PACK)
-                nc.tensor.transpose(
-                    out=normed_t[c][:, P * t : P * (t + 1)], in_=normed[:, P * r : P * (r + 1)], identity=identity[:]
-                )
-            h2_planes[i] = packs.tile([P, PACK, PASSES * P], BF16, name="h2_planes")
-            for r in range(K_ROWS):
-                c, t = divmod(r, PACK)
-                nc.scalar.activation(
-                    out=h2_planes[i][:, t, P * c : P * (c + 1)], in_=normed_t[c][:, P * t : P * (t + 1)],
-                    func=ACT.Identity, scale=gain_bias[:, r : r + 1], bias=gain_bias[:, K_ROWS + r : K_ROWS + r + 1],
-                )
+        def normalise_and_transpose(q):
+            normed = []
+            for i in range(PAIR * q, PAIR * (q + 1)):
+                tile = row("normed")
+                normed.append(tile)
+                for c in range(PASSES):
+                    cols = slice(K_PASS * c, K_PASS * (c + 1))
+                    nc.vector.tensor_scalar(
+                        out=tile[:, cols].rearrange("n (t b i) -> n t b i", t=PACK, i=RUN_K),
+                        in0=x_mid[i][:, cols].rearrange("n (b t i) -> n t b i", t=PACK, i=RUN_K),
+                        scalar1=neg_mean[:, i : i + 1], scalar2=rstd[:, i : i + 1], op0=ALU.add, op1=ALU.mult,
+                    )
+            h2_planes[q] = packs.tile([P, PACK, PASSES * PAIR_TOKENS], BF16, name="h2_planes")
+            for half in range(K_ROWS // 2):
+                normed_t = bank("normed_t")
+                for s in range(2):
+                    r = 2 * half + s
+                    for m in range(PAIR):
+                        nc.tensor.transpose(
+                            out=normed_t[:, PAIR_TOKENS * s + P * m : PAIR_TOKENS * s + P * (m + 1)],
+                            in_=normed[m][:, P * r : P * (r + 1)], identity=identity[:],
+                        )
+                for s in range(2):
+                    r = 2 * half + s
+                    c, t = divmod(r, PACK)
+                    nc.scalar.activation(
+                        out=h2_planes[q][:, t, PAIR_TOKENS * c : PAIR_TOKENS * (c + 1)],
+                        in_=normed_t[:, PAIR_TOKENS * s : PAIR_TOKENS * (s + 1)],
+                        func=ACT.Identity, scale=gain_bias[:, r : r + 1], bias=gain_bias[:, K_ROWS + r : K_ROWS + r + 1],
+                    )
 
-        def regroup_h2(i):
-            h2_grouped[i] = packs.tile([P, PACK * PASSES * P], BF16, name="h2_grouped", align_bytes=64)
-            regroup(nc.vector.tensor_copy, h2_grouped[i][:], h2_planes[i][:])
+        def regroup_h2(q):
+            h2_grouped[q] = packs.tile([P, PACK * PASSES * PAIR_TOKENS], BF16, name="h2_grouped", align_bytes=64)
+            regroup(nc.vector.tensor_copy, h2_grouped[q][:], h2_planes[q][:])
 
-        def quantise_h2(i):
-            quantise(h2_grouped[i][:], h2_words[:, i, :], h2_scales[:, i, :])
+        def quantise_h2(q):
+            quantise(h2_grouped[q][:], h2_words[:, q, :], h2_scales[:, q, :])
 
-        def hid_matmul(j, i):
-            hid_acc[(j, i)] = [bank("acc2_%d" % n) for n in range(CHUNK // BANK)]
-            for n in range(CHUNK // BANK):
-                cols = slice(CHUNK * j + BANK * n, CHUNK * j + BANK * (n + 1))
-                multiply(hid_acc[(j, i)][n][:], h2_words, h2_scales, i, w1_words, w1_scales, cols)
+        def hid_tile(j, i, banks_at_a_time):
+            q, m = divmod(i, PAIR)
 
-        def hid_finish(j, i, banks_at_a_time):
+            def words_of_pass(c):
+                tokens = slice(PAIR_TOKENS * c + P * m, PAIR_TOKENS * c + P * (m + 1))
+                return h2_words[:, q, tokens], h2_scales[:, q, tokens]
+
             hid = row("hid")
             for first in range(0, CHUNK // BANK, banks_at_a_time):
                 for n in range(first, first + banks_at_a_time):
+                    cols = slice(CHUNK * j + BANK * n, CHUNK * j + BANK * (n + 1))
+                    acc = bank("acc2")
+                    multiply(acc[:], words_of_pass, w1_words, w1_scales, cols)
                     nc.vector.tensor_tensor(
-                        out=hid[:, BANK * n : BANK * (n + 1)], in0=hid_acc[(j, i)][n][:],
-                        in1=b1_all[:, CHUNK * j + BANK * n : CHUNK * j + BANK * (n + 1)], op=ALU.add,
+                        out=hid[:, BANK * n : BANK * (n + 1)], in0=acc[:], in1=b1_all[:, cols], op=ALU.add
                     )
                 part = slice(BANK * first, BANK * (first + banks_at_a_time))
                 nc.scalar.activation(out=hid[:, part], in_=hid[:, part], func=ACT.Gelu)
@@ -338,19 +315,46 @@ def tile_transformerblock_pb_kernel(tc, attn, x, w_out, b_out, ln2_g, ln2_b, w1,
                     in_=hid[:, part],
                 )
 
-        for r in range(TOKEN_TILES + 3):
-            if r < TOKEN_TILES:
-                normalise_and_transpose(r)
-            if 2 <= r < TOKEN_TILES + 2:
+        for i in range(PAIR):
+            transpose_attn(i)
+        for i in range(PAIR):
+            add_b_out(i)
+            quantise_attn(i)
+        next_piece = 0
+        for r in range(PAIRS + 3):
+            if r < PAIRS:
+                for i in range(PAIR * r, PAIR * (r + 1)):
+                    project(i)
+                    if i + PAIR < TOKEN_TILES:
+                        transpose_attn(i + PAIR)
+                        add_b_out(i + PAIR)
+                if r + 1 < PAIRS:
+                    for i in range(PAIR * (r + 1), PAIR * (r + 2)):
+                        quantise_attn(i)
+                rstd_of_pair(r)
+            if r == 0:
+                prepare_gain_bias()
+            if r >= 2:
+                prepare_w1(next_piece)
+                prepare_w1(next_piece + 1)
+                next_piece += 2
+            if r in (1, 4):
+                load_w1_chunk(2 if r == 1 else 3)
+            if 1 <= r <= PAIRS:
+                normalise_and_transpose(r - 1)
+            if r == 3:
+                prepare_w1(next_piece)
+                next_piece += 1
+            if 2 <= r <= PAIRS + 1:
                 regroup_h2(r - 2)
-            prepare_w1(PIECES_PER_CHUNK + FILL + r)
-            if 2 <= r < TOKEN_TILES + 2:
                 quantise_h2(r - 2)
-                hid_matmul(0, r - 2)
             if r >= 3:
-                hid_finish(0, r - 3, CHUNK // BANK)
+                for i in range(PAIR * (r - 3), PAIR * (r - 2)):
+                    hid_tile(0, i, CHUNK // BANK)
         for j in range(1, CHUNKS):
             for i in range(TOKEN_TILES):
+                if next_piece <= W1_PIECES:
+                    prepare_w1(next_piece)
+                    next_piece += 1
                 last = j == CHUNKS - 1 and i == TOKEN_TILES - 1
-                hid_matmul(j, i)
-                hid_finish(j, i, 1 if last else CHUNK // BANK)
+                hid_tile(j, i, 1 if last else CHUNK // BANK)

@@ -16,7 +16,9 @@ PACK = 4
 K_PASS = P * PACK
 BANK = 512
 RAW_BUFS = 3
-SCALAR_PIECES = (3, 5, 7, 9, 11)
+C0_AFTER = 1
+VECTOR_BIAS_TILES = 2
+SCALAR_PIECES = (3, 5, 7, 9, 11, 13, 15)
 RUN_K = 8
 RUN = 4
 
@@ -59,6 +61,7 @@ def tile_transformerblock_pb_kernel(tc, attn, x, w_out, b_out, ln2_g, ln2_b, w1,
         keep = ctx.enter_context(tc.tile_pool(name="keep", bufs=1))
         raw = ctx.enter_context(tc.tile_pool(name="raw", bufs=RAW_BUFS))
         pieces = ctx.enter_context(tc.tile_pool(name="pieces", bufs=3))
+        attn_packs = ctx.enter_context(tc.tile_pool(name="attn_packs", bufs=3))
         packs = ctx.enter_context(tc.tile_pool(name="packs", bufs=2))
         rows = ctx.enter_context(tc.tile_pool(name="rows", bufs=13))
         psum = ctx.enter_context(tc.psum_pool(name="psum", bufs=8))
@@ -83,14 +86,6 @@ def tile_transformerblock_pb_kernel(tc, attn, x, w_out, b_out, ln2_g, ln2_b, w1,
                         out=w1_raw[j][:, PACK * c + t, :], in_=w1_rows[c, t, :, :, CHUNK * j : CHUNK * (j + 1)]
                     )
 
-        w_out_raw = raw_tile("w_out_raw")
-        for g in range(PASSES):
-            nc.sync.dma_start(out=w_out_raw[:, PACK * g : PACK * (g + 1), :], in_=w_out_rows[g])
-        attn_raw = raw_tile("attn_raw")
-        x_raw = keep.tile([P, TOKEN_TILES, WIDTH], BF16, name="x_raw")
-        for tiles in (slice(0, PAIR), slice(PAIR, TOKEN_TILES)):
-            nc.sync.dma_start(out=attn_raw[:, tiles, :], in_=attn_rows[:, tiles, :])
-            nc.sync.dma_start(out=x_raw[:, tiles, :], in_=x_rows[:, tiles, :])
         gain_bias_rows = keep.tile([P, P], BF16, name="gain_bias_rows")
         nc.vector.memset(gain_bias_rows[:], 0.0)
         for v, vector in enumerate((ln2_g, ln2_b)):
@@ -100,7 +95,18 @@ def tile_transformerblock_pb_kernel(tc, attn, x, w_out, b_out, ln2_g, ln2_b, w1,
                 nc.sync.dma_start(
                     out=gain_bias_rows[first : first + PACK, :].rearrange("t (b i) -> t b i", i=RUN_K), in_=vector_rows[c]
                 )
-        load_w1_chunk(0)
+        w_out_raw = raw_tile("w_out_raw")
+        w_out_pieces = [(g, slice(PIECE * n, PIECE * (n + 1))) for g in range(PASSES) for n in range(WIDTH // PIECE)]
+        for g, cols in w_out_pieces:
+            nc.sync.dma_start(out=w_out_raw[:, PACK * g : PACK * (g + 1), cols], in_=w_out_rows[g, :, :, cols])
+        attn_raw = raw_tile("attn_raw")
+        x_raw = keep.tile([P, TOKEN_TILES, WIDTH], BF16, name="x_raw")
+        for q in range(PAIRS):
+            tiles = slice(PAIR * q, PAIR * (q + 1))
+            nc.sync.dma_start(out=attn_raw[:, tiles, :], in_=attn_rows[:, tiles, :])
+            nc.sync.dma_start(out=x_raw[:, tiles, :], in_=x_rows[:, tiles, :])
+            if q == C0_AFTER:
+                load_w1_chunk(0)
         load_w1_chunk(1)
         b1_all = keep.tile([P, HIDDEN], BF16, name="b1_all")
         nc.sync.dma_start(out=b1_all[:], in_=b1.partition_broadcast(P))
@@ -115,6 +121,20 @@ def tile_transformerblock_pb_kernel(tc, attn, x, w_out, b_out, ln2_g, ln2_b, w1,
         nc.vector.tensor_copy(out=identity_bf16[:], in_=identity[:])
         ones = keep.tile([P, P], BF16, name="ones")
         nc.vector.memset(ones[:], 1.0)
+        b_out_all = keep.tile([P, WIDTH], BF16, name="b_out_all")
+        for n in range(WIDTH // BANK):
+            cols = slice(BANK * n, BANK * (n + 1))
+            spread = bank("spread")
+            nc.tensor.matmul(out=spread[:], lhsT=ones[:], rhs=b_out_row[:, cols], start=True, stop=True)
+            nc.scalar.copy(out=b_out_all[:, cols], in_=spread[:])
+
+        gain_bias = keep.tile([P, 2 * K_ROWS], F32, name="gain_bias")
+
+        gain_bias_f32 = keep.tile([P, P], F32, name="gain_bias_f32")
+        nc.vector.tensor_copy(out=gain_bias_f32[:], in_=gain_bias_rows[:])
+        gain_bias_t = bank("gain_bias_t")
+        nc.tensor.transpose(out=gain_bias_t[:, 0:P], in_=gain_bias_f32[:], identity=identity[:])
+        nc.vector.tensor_copy(out=gain_bias[:], in_=gain_bias_t[:, 0 : 2 * K_ROWS])
 
         def quantised(name, outer, width):
             words = keep.tile([P, outer, width], U32, name=name + "_words", align_bytes=64)
@@ -158,7 +178,6 @@ def tile_transformerblock_pb_kernel(tc, attn, x, w_out, b_out, ln2_g, ln2_b, w1,
                 j, c, cols, cols_in_chunk = w1_piece(k - 1)
                 quantise(piece_tiles[("w1", k - 1)][:], w1_words[:, c, cols], w1_scales[:, c, cols])
 
-        w_out_pieces = [(g, slice(PIECE * n, PIECE * (n + 1))) for g in range(PASSES) for n in range(WIDTH // PIECE)]
         for k in range(len(w_out_pieces) + 1):
             if k < len(w_out_pieces):
                 g, cols = w_out_pieces[k]
@@ -180,7 +199,7 @@ def tile_transformerblock_pb_kernel(tc, attn, x, w_out, b_out, ln2_g, ln2_b, w1,
                         in_=attn_pairs[:, 2 * P * g + u : 2 * P * (g + 1) : 2],
                         identity=identity[:],
                     )
-            attn_grouped[i] = packs.tile([P, PACK * PASSES * P], BF16, name="attn_grouped", align_bytes=64)
+            attn_grouped[i] = attn_packs.tile([P, PACK * PASSES * P], BF16, name="attn_grouped", align_bytes=64)
             nc.scalar.copy(
                 out=attn_grouped[i][:].bitcast(F32).rearrange("q (m u) -> q m u", u=2),
                 in_=attn_t[:].rearrange("q (u m) -> q m u", u=2),
@@ -204,6 +223,9 @@ def tile_transformerblock_pb_kernel(tc, attn, x, w_out, b_out, ln2_g, ln2_b, w1,
 
         def add_b_out(i):
             x_bias[i] = row("x_bias")
+            if i < VECTOR_BIAS_TILES:
+                nc.vector.tensor_tensor(out=x_bias[i][:], in0=x_raw[:, i, :], in1=b_out_all[:], op=ALU.add)
+                return
             for n in range(WIDTH // BANK):
                 cols = slice(BANK * n, BANK * (n + 1))
                 sums = bank("x_bias_sums")
@@ -226,6 +248,8 @@ def tile_transformerblock_pb_kernel(tc, attn, x, w_out, b_out, ln2_g, ln2_b, w1,
                     op0=ALU.mult, op1=ALU.add, accum_out=row_sums[:, i, n : n + 1],
                 )
             nc.sync.dma_start(out=x_mid_rows[:, i, :], in_=x_mid[i][:])
+
+        def row_statistics(i):
             nc.scalar.activation(
                 out=scaled_sums[:], in_=row_sums[:, i, :], func=ACT.Identity, scale=-1.0 / WIDTH,
                 accum_out=neg_mean[:, i : i + 1],
@@ -242,30 +266,22 @@ def tile_transformerblock_pb_kernel(tc, attn, x, w_out, b_out, ln2_g, ln2_b, w1,
             )
             nc.gpsimd.tensor_tensor(out=rstd[:, tiles], in0=var_eps[:, tiles], in1=neg_half[:], op=ALU.pow)
 
-        gain_bias = keep.tile([P, 2 * K_ROWS], F32, name="gain_bias")
-
-        def prepare_gain_bias():
-            gain_bias_f32 = keep.tile([P, P], F32, name="gain_bias_f32")
-            nc.vector.tensor_copy(out=gain_bias_f32[:], in_=gain_bias_rows[:])
-            gain_bias_t = bank("gain_bias_t")
-            nc.tensor.transpose(out=gain_bias_t[:, 0:P], in_=gain_bias_f32[:], identity=identity[:])
-            nc.vector.tensor_copy(out=gain_bias[:], in_=gain_bias_t[:, 0 : 2 * K_ROWS])
-
         h2_planes = {}
         h2_grouped = {}
 
-        def normalise_and_transpose(q):
-            normed = []
-            for i in range(PAIR * q, PAIR * (q + 1)):
-                tile = row("normed")
-                normed.append(tile)
-                for c in range(PASSES):
-                    cols = slice(K_PASS * c, K_PASS * (c + 1))
-                    nc.vector.tensor_scalar(
-                        out=tile[:, cols].rearrange("n (t b i) -> n t b i", t=PACK, i=RUN_K),
-                        in0=x_mid[i][:, cols].rearrange("n (b t i) -> n t b i", t=PACK, i=RUN_K),
-                        scalar1=neg_mean[:, i : i + 1], scalar2=rstd[:, i : i + 1], op0=ALU.add, op1=ALU.mult,
-                    )
+        normed = {}
+
+        def normalise(i):
+            normed[i] = row("normed")
+            for c in range(PASSES):
+                cols = slice(K_PASS * c, K_PASS * (c + 1))
+                nc.vector.tensor_scalar(
+                    out=normed[i][:, cols].rearrange("n (t b i) -> n t b i", t=PACK, i=RUN_K),
+                    in0=x_mid[i][:, cols].rearrange("n (b t i) -> n t b i", t=PACK, i=RUN_K),
+                    scalar1=neg_mean[:, i : i + 1], scalar2=rstd[:, i : i + 1], op0=ALU.add, op1=ALU.mult,
+                )
+
+        def transpose_normed(q):
             h2_planes[q] = packs.tile([P, PACK, PASSES * PAIR_TOKENS], BF16, name="h2_planes")
             for half in range(K_ROWS // 2):
                 normed_t = bank("normed_t")
@@ -274,7 +290,7 @@ def tile_transformerblock_pb_kernel(tc, attn, x, w_out, b_out, ln2_g, ln2_b, w1,
                     for m in range(PAIR):
                         nc.tensor.transpose(
                             out=normed_t[:, PAIR_TOKENS * s + P * m : PAIR_TOKENS * s + P * (m + 1)],
-                            in_=normed[m][:, P * r : P * (r + 1)], identity=identity[:],
+                            in_=normed[PAIR * q + m][:, P * r : P * (r + 1)], identity=identity[:],
                         )
                 for s in range(2):
                     r = 2 * half + s
@@ -292,69 +308,66 @@ def tile_transformerblock_pb_kernel(tc, attn, x, w_out, b_out, ln2_g, ln2_b, w1,
         def quantise_h2(q):
             quantise(h2_grouped[q][:], h2_words[:, q, :], h2_scales[:, q, :])
 
-        def hid_tile(j, i, banks_at_a_time):
+        hid = {}
+
+        def hid_multiply(j, i):
             q, m = divmod(i, PAIR)
 
             def words_of_pass(c):
                 tokens = slice(PAIR_TOKENS * c + P * m, PAIR_TOKENS * c + P * (m + 1))
                 return h2_words[:, q, tokens], h2_scales[:, q, tokens]
 
-            hid = row("hid")
-            for first in range(0, CHUNK // BANK, banks_at_a_time):
-                for n in range(first, first + banks_at_a_time):
-                    cols = slice(CHUNK * j + BANK * n, CHUNK * j + BANK * (n + 1))
-                    acc = bank("acc2")
-                    multiply(acc[:], words_of_pass, w1_words, w1_scales, cols)
-                    nc.vector.tensor_tensor(
-                        out=hid[:, BANK * n : BANK * (n + 1)], in0=acc[:], in1=b1_all[:, cols], op=ALU.add
-                    )
-                part = slice(BANK * first, BANK * (first + banks_at_a_time))
-                nc.scalar.activation(out=hid[:, part], in_=hid[:, part], func=ACT.Gelu)
-                nc.sync.dma_start(
-                    out=hid_rows[:, i, CHUNK * j + BANK * first : CHUNK * j + BANK * (first + banks_at_a_time)],
-                    in_=hid[:, part],
+            hid[i] = row("hid")
+            for n in range(CHUNK // BANK):
+                cols = slice(CHUNK * j + BANK * n, CHUNK * j + BANK * (n + 1))
+                acc = bank("acc2")
+                multiply(acc[:], words_of_pass, w1_words, w1_scales, cols)
+                nc.vector.tensor_tensor(
+                    out=hid[i][:, BANK * n : BANK * (n + 1)], in0=acc[:], in1=b1_all[:, cols], op=ALU.add
                 )
 
+        def hid_finish(j, i, width):
+            for first in range(0, CHUNK, width):
+                part = hid[i][:, first : first + width]
+                nc.scalar.activation(out=part, in_=part, func=ACT.Gelu)
+                nc.sync.dma_start(
+                    out=hid_rows[:, i, CHUNK * j + first : CHUNK * j + first + width], in_=part
+                )
+
+        ctx.enter_context(tc.manual_schedule())
         for i in range(PAIR):
             transpose_attn(i)
         for i in range(PAIR):
             add_b_out(i)
             quantise_attn(i)
-        next_piece = 0
-        for r in range(PAIRS + 3):
-            if r < PAIRS:
-                for i in range(PAIR * r, PAIR * (r + 1)):
-                    project(i)
-                    if i + PAIR < TOKEN_TILES:
-                        transpose_attn(i + PAIR)
-                        add_b_out(i + PAIR)
-                if r + 1 < PAIRS:
-                    for i in range(PAIR * (r + 1), PAIR * (r + 2)):
-                        quantise_attn(i)
-                rstd_of_pair(r)
-            if r == 0:
-                prepare_gain_bias()
-            if r >= 2:
-                prepare_w1(next_piece)
-                prepare_w1(next_piece + 1)
-                next_piece += 2
-            if r in (1, 4):
-                load_w1_chunk(2 if r == 1 else 3)
-            if 1 <= r <= PAIRS:
-                normalise_and_transpose(r - 1)
-            if r == 3:
-                prepare_w1(next_piece)
-                next_piece += 1
-            if 2 <= r <= PAIRS + 1:
-                regroup_h2(r - 2)
-                quantise_h2(r - 2)
-            if r >= 3:
-                for i in range(PAIR * (r - 3), PAIR * (r - 2)):
-                    hid_tile(0, i, CHUNK // BANK)
-        for j in range(1, CHUNKS):
-            for i in range(TOKEN_TILES):
-                if next_piece <= W1_PIECES:
-                    prepare_w1(next_piece)
-                    next_piece += 1
-                last = j == CHUNKS - 1 and i == TOKEN_TILES - 1
-                hid_tile(j, i, 1 if last else CHUNK // BANK)
+        pieces_done = 0
+        for s in range(TOKEN_TILES * (CHUNKS + 1)):
+            if s + PAIR < TOKEN_TILES:
+                transpose_attn(s + PAIR)
+                add_b_out(s + PAIR)
+            if s < TOKEN_TILES:
+                project(s)
+            if s + PAIR < TOKEN_TILES:
+                quantise_attn(s + PAIR)
+            if 1 <= s < TOKEN_TILES + 1:
+                row_statistics(s - 1)
+                if s % PAIR == 0:
+                    rstd_of_pair(s // PAIR - 1)
+            if 3 <= s < TOKEN_TILES + 3:
+                normalise(s - 3)
+            if s % PAIR == 1 and 5 <= s < TOKEN_TILES + 5:
+                transpose_normed((s - 5) // PAIR)
+            if pieces_done <= W1_PIECES and s in (2,3,4,6,7,8,10,12,14,16,18,20,22,24,26,28,30):
+                prepare_w1(pieces_done)
+                pieces_done += 1
+            if s in (6, 10):
+                load_w1_chunk(2 if s == 6 else 3)
+            if s % PAIR == 0 and 6 <= s < TOKEN_TILES + 6:
+                regroup_h2((s - 6) // PAIR)
+            if s % PAIR == 1 and 7 <= s < TOKEN_TILES + 7:
+                quantise_h2((s - 7) // PAIR)
+            if s >= 8:
+                hid_multiply((s - 8) // TOKEN_TILES, s % TOKEN_TILES)
+            if s >= 9:
+                hid_finish((s - 9) // TOKEN_TILES, (s - 9) % TOKEN_TILES, CHUNK)
+        hid_finish(CHUNKS - 1, TOKEN_TILES - 1, BANK)

@@ -16,6 +16,7 @@ PACK = 4
 K_PASS = P * PACK
 BANK = 512
 RAW_BUFS = 3
+ROW_BUFS = 20
 C0_AFTER = 1
 VECTOR_BIAS_TILES = 2
 SCALAR_PIECES = (3, 5, 7, 9, 11, 13, 15)
@@ -31,6 +32,7 @@ K_ROWS = WIDTH // P
 PASSES = WIDTH // K_PASS
 CHUNK = 1024
 CHUNKS = HIDDEN // CHUNK
+HALF = HIDDEN // 2
 PIECE = BANK
 PIECES_PER_CHUNK = PASSES * (CHUNK // PIECE)
 W1_PIECES = CHUNKS * PIECES_PER_CHUNK
@@ -60,10 +62,9 @@ def tile_transformerblock_pb_kernel(tc, attn, x, w_out, b_out, ln2_g, ln2_b, w1,
     with ExitStack() as ctx:
         keep = ctx.enter_context(tc.tile_pool(name="keep", bufs=1))
         raw = ctx.enter_context(tc.tile_pool(name="raw", bufs=RAW_BUFS))
-        pieces = ctx.enter_context(tc.tile_pool(name="pieces", bufs=3))
         attn_packs = ctx.enter_context(tc.tile_pool(name="attn_packs", bufs=3))
         packs = ctx.enter_context(tc.tile_pool(name="packs", bufs=2))
-        rows = ctx.enter_context(tc.tile_pool(name="rows", bufs=13))
+        rows = ctx.enter_context(tc.tile_pool(name="rows", bufs=ROW_BUFS))
         psum = ctx.enter_context(tc.psum_pool(name="psum", bufs=8))
 
         def bank(name):
@@ -78,13 +79,11 @@ def tile_transformerblock_pb_kernel(tc, attn, x, w_out, b_out, ln2_g, ln2_b, w1,
 
         w1_raw = {}
 
-        def load_w1_chunk(j):
-            w1_raw[j] = raw_tile("w1_raw%d" % j)
-            for c in range(PASSES):
-                for t in range(PACK):
-                    nc.sync.dma_start(
-                        out=w1_raw[j][:, PACK * c + t, :], in_=w1_rows[c, t, :, :, CHUNK * j : CHUNK * (j + 1)]
-                    )
+        def load_w1(load):
+            half, c = divmod(load, PASSES)
+            w1_raw[load] = raw.tile([P, PACK, HALF], BF16, name="w1_raw%d" % load, tag="raw")
+            for t in range(PACK):
+                nc.sync.dma_start(out=w1_raw[load][:, t, :], in_=w1_rows[c, t, :, :, HALF * half : HALF * (half + 1)])
 
         gain_bias_rows = keep.tile([P, P], BF16, name="gain_bias_rows")
         nc.vector.memset(gain_bias_rows[:], 0.0)
@@ -100,14 +99,15 @@ def tile_transformerblock_pb_kernel(tc, attn, x, w_out, b_out, ln2_g, ln2_b, w1,
         for g, cols in w_out_pieces:
             nc.sync.dma_start(out=w_out_raw[:, PACK * g : PACK * (g + 1), cols], in_=w_out_rows[g, :, :, cols])
         attn_raw = raw_tile("attn_raw")
-        x_raw = keep.tile([P, TOKEN_TILES, WIDTH], BF16, name="x_raw")
+        x_raw = {}
         for q in range(PAIRS):
             tiles = slice(PAIR * q, PAIR * (q + 1))
             nc.sync.dma_start(out=attn_raw[:, tiles, :], in_=attn_rows[:, tiles, :])
-            nc.sync.dma_start(out=x_raw[:, tiles, :], in_=x_rows[:, tiles, :])
+            x_raw[q] = rows.tile([P, PAIR, WIDTH], BF16, name="x_raw", tag="row", align_bytes=64)
+            nc.sync.dma_start(out=x_raw[q][:], in_=x_rows[:, tiles, :])
             if q == C0_AFTER:
-                load_w1_chunk(0)
-        load_w1_chunk(1)
+                load_w1(0)
+        load_w1(1)
         b1_all = keep.tile([P, HIDDEN], BF16, name="b1_all")
         nc.sync.dma_start(out=b1_all[:], in_=b1.partition_broadcast(P))
 
@@ -161,21 +161,22 @@ def tile_transformerblock_pb_kernel(tc, attn, x, w_out, b_out, ln2_g, ln2_b, w1,
         piece_tiles = {}
 
         def regroup_piece(key, copy, raw_rows):
-            piece_tiles[key] = pieces.tile([P, PACK * PIECE], BF16, name="piece", tag="piece", align_bytes=64)
+            piece_tiles[key] = rows.tile([P, PACK * PIECE], BF16, name="piece", tag="row", align_bytes=64)
             regroup(copy, piece_tiles[key][:], raw_rows)
 
         def w1_piece(k):
-            j, rest = divmod(k, PIECES_PER_CHUNK)
-            c, n = divmod(rest, CHUNK // PIECE)
-            return j, c, slice(CHUNK * j + PIECE * n, CHUNK * j + PIECE * (n + 1)), slice(PIECE * n, PIECE * (n + 1))
+            load, n = divmod(k, HALF // PIECE)
+            half, c = divmod(load, PASSES)
+            first = HALF * half + PIECE * n
+            return load, c, slice(first, first + PIECE), slice(PIECE * n, PIECE * (n + 1))
 
         def prepare_w1(k):
             if k < W1_PIECES:
-                j, c, cols, cols_in_chunk = w1_piece(k)
+                load, c, cols, cols_in_load = w1_piece(k)
                 copy = nc.scalar.copy if k in SCALAR_PIECES else nc.vector.tensor_copy
-                regroup_piece(("w1", k), copy, w1_raw[j][:, PACK * c : PACK * (c + 1), cols_in_chunk])
+                regroup_piece(("w1", k), copy, w1_raw[load][:, :, cols_in_load])
             if 1 <= k <= W1_PIECES:
-                j, c, cols, cols_in_chunk = w1_piece(k - 1)
+                load, c, cols, cols_in_load = w1_piece(k - 1)
                 quantise(piece_tiles[("w1", k - 1)][:], w1_words[:, c, cols], w1_scales[:, c, cols])
 
         for k in range(len(w_out_pieces) + 1):
@@ -209,7 +210,7 @@ def tile_transformerblock_pb_kernel(tc, attn, x, w_out, b_out, ln2_g, ln2_b, w1,
             quantise(attn_grouped[i][:], attn_words[:, i, :], attn_scales[:, i, :])
 
         def row(name):
-            return rows.tile([P, WIDTH], F32, name=name, tag="row")
+            return rows.tile([P, WIDTH], F32, name=name, tag="row", align_bytes=64)
 
         x_bias = {}
         x_mid = {}
@@ -222,14 +223,15 @@ def tile_transformerblock_pb_kernel(tc, attn, x, w_out, b_out, ln2_g, ln2_b, w1,
         rstd = keep.tile([P, TOKEN_TILES], F32, name="rstd")
 
         def add_b_out(i):
+            x_tile = x_raw[i // PAIR][:, i % PAIR, :]
             x_bias[i] = row("x_bias")
             if i < VECTOR_BIAS_TILES:
-                nc.vector.tensor_tensor(out=x_bias[i][:], in0=x_raw[:, i, :], in1=b_out_all[:], op=ALU.add)
+                nc.vector.tensor_tensor(out=x_bias[i][:], in0=x_tile, in1=b_out_all[:], op=ALU.add)
                 return
             for n in range(WIDTH // BANK):
                 cols = slice(BANK * n, BANK * (n + 1))
                 sums = bank("x_bias_sums")
-                nc.tensor.matmul(out=sums[:], lhsT=identity_bf16[:], rhs=x_raw[:, i, cols], start=True, stop=False)
+                nc.tensor.matmul(out=sums[:], lhsT=identity_bf16[:], rhs=x_tile[:, cols], start=True, stop=False)
                 nc.tensor.matmul(out=sums[:], lhsT=ones[:], rhs=b_out_row[:, cols], start=False, stop=True)
                 nc.scalar.copy(out=x_bias[i][:, cols], in_=sums[:])
 
@@ -341,7 +343,7 @@ def tile_transformerblock_pb_kernel(tc, attn, x, w_out, b_out, ln2_g, ln2_b, w1,
             add_b_out(i)
             quantise_attn(i)
         pieces_done = 0
-        for s in range(TOKEN_TILES * (CHUNKS + 1)):
+        for s in range(TOKEN_TILES * CHUNKS + 9):
             if s + PAIR < TOKEN_TILES:
                 transpose_attn(s + PAIR)
                 add_b_out(s + PAIR)
@@ -353,21 +355,21 @@ def tile_transformerblock_pb_kernel(tc, attn, x, w_out, b_out, ln2_g, ln2_b, w1,
                 row_statistics(s - 1)
                 if s % PAIR == 0:
                     rstd_of_pair(s // PAIR - 1)
-            if 3 <= s < TOKEN_TILES + 3:
-                normalise(s - 3)
-            if s % PAIR == 1 and 5 <= s < TOKEN_TILES + 5:
-                transpose_normed((s - 5) // PAIR)
-            if pieces_done <= W1_PIECES and s in (2,3,4,6,7,8,10,12,14,16,18,20,22,24,26,28,30):
+            if 4 <= s < TOKEN_TILES + 4:
+                normalise(s - 4)
+            if (s - 4) % PAIR == 0 and 6 <= s < TOKEN_TILES + 6:
+                transpose_normed((s - 6) // PAIR)
+            if pieces_done <= W1_PIECES and s in (2, 3, 4, 5, 6, 7, 8, 9, 12, 14, 16, 18, 20, 22, 24, 26, 28):
                 prepare_w1(pieces_done)
                 pieces_done += 1
-            if s in (6, 10):
-                load_w1_chunk(2 if s == 6 else 3)
-            if s % PAIR == 0 and 6 <= s < TOKEN_TILES + 6:
-                regroup_h2((s - 6) // PAIR)
-            if s % PAIR == 1 and 7 <= s < TOKEN_TILES + 7:
-                quantise_h2((s - 7) // PAIR)
-            if s >= 8:
-                hid_multiply((s - 8) // TOKEN_TILES, s % TOKEN_TILES)
+            if s in (6, 9):
+                load_w1(2 if s == 6 else 3)
+            if (s - 7) % PAIR == 0 and 7 <= s < TOKEN_TILES + 7:
+                regroup_h2((s - 7) // PAIR)
+            if (s - 8) % PAIR == 0 and 8 <= s < TOKEN_TILES + 8:
+                quantise_h2((s - 8) // PAIR)
             if s >= 9:
-                hid_finish((s - 9) // TOKEN_TILES, (s - 9) % TOKEN_TILES, CHUNK)
+                hid_multiply((s - 9) // TOKEN_TILES, (s - 9) % TOKEN_TILES)
+            if s >= 10:
+                hid_finish((s - 10) // TOKEN_TILES, (s - 10) % TOKEN_TILES, CHUNK)
         hid_finish(CHUNKS - 1, TOKEN_TILES - 1, BANK)

@@ -67,12 +67,10 @@ def tile_transformerblock_pb_kernel(tc, attn, x, w_out, b_out, ln2_g, ln2_b, w1,
         rows = ctx.enter_context(tc.tile_pool(name="rows", bufs=ROW_BUFS))
         psum = ctx.enter_context(tc.psum_pool(name="psum", bufs=8))
 
+        ctx.enter_context(tc.manual_schedule())
+
         def bank(name):
             return psum.tile([P, BANK], F32, name=name, tag="bank")
-
-        b_out_row = keep.tile([P, WIDTH], BF16, name="b_out_row")
-        nc.vector.memset(b_out_row[:], 0.0)
-        nc.sync.dma_start(out=b_out_row[0:1, :], in_=b_out.rearrange("(o d) -> o d", o=1))
 
         def raw_tile(name):
             return raw.tile([P, PASSES * PACK, CHUNK], BF16, name=name, tag="raw")
@@ -85,6 +83,18 @@ def tile_transformerblock_pb_kernel(tc, attn, x, w_out, b_out, ln2_g, ln2_b, w1,
             for t in range(PACK):
                 nc.sync.dma_start(out=w1_raw[load][:, t, :], in_=w1_rows[c, t, :, :, HALF * half : HALF * (half + 1)])
 
+        w_out_raw = raw_tile("w_out_raw")
+        w_out_pieces = [(g, slice(PIECE * n, PIECE * (n + 1))) for g in range(PASSES) for n in range(WIDTH // PIECE)]
+
+        def load_w_out(piece):
+            g, cols = piece
+            nc.sync.dma_start(out=w_out_raw[:, PACK * g : PACK * (g + 1), cols], in_=w_out_rows[g, :, :, cols])
+
+        load_w_out(w_out_pieces[0])
+        b_out_row = keep.tile([P, WIDTH], BF16, name="b_out_row")
+        nc.vector.memset(b_out_row[:], 0.0)
+        nc.sync.dma_start(out=b_out_row[0:1, :], in_=b_out.rearrange("(o d) -> o d", o=1))
+
         gain_bias_rows = keep.tile([P, P], BF16, name="gain_bias_rows")
         nc.vector.memset(gain_bias_rows[:], 0.0)
         for v, vector in enumerate((ln2_g, ln2_b)):
@@ -94,10 +104,8 @@ def tile_transformerblock_pb_kernel(tc, attn, x, w_out, b_out, ln2_g, ln2_b, w1,
                 nc.sync.dma_start(
                     out=gain_bias_rows[first : first + PACK, :].rearrange("t (b i) -> t b i", i=RUN_K), in_=vector_rows[c]
                 )
-        w_out_raw = raw_tile("w_out_raw")
-        w_out_pieces = [(g, slice(PIECE * n, PIECE * (n + 1))) for g in range(PASSES) for n in range(WIDTH // PIECE)]
-        for g, cols in w_out_pieces:
-            nc.sync.dma_start(out=w_out_raw[:, PACK * g : PACK * (g + 1), cols], in_=w_out_rows[g, :, :, cols])
+        for piece in w_out_pieces[1:]:
+            load_w_out(piece)
         attn_raw = raw_tile("attn_raw")
         x_raw = {}
         for q in range(PAIRS):
@@ -336,7 +344,6 @@ def tile_transformerblock_pb_kernel(tc, attn, x, w_out, b_out, ln2_g, ln2_b, w1,
                     out=hid_rows[:, i, CHUNK * j + first : CHUNK * j + first + width], in_=part
                 )
 
-        ctx.enter_context(tc.manual_schedule())
         for i in range(PAIR):
             transpose_attn(i)
         for i in range(PAIR):

@@ -17,10 +17,9 @@ K_PASS = P * PACK
 BANK = 512
 RAW_BUFS = 3
 ROW_BUFS = 20
-C0_AFTER = 1
-VECTOR_BIAS_TILES = 2
+C0_AFTER = 2
+VECTOR_BIAS_TILES = 4
 SCALAR_PIECES = (3, 5, 7, 9, 11, 13, 15)
-RUN_K = 8
 RUN = 4
 
 TOKENS = 1024
@@ -57,7 +56,7 @@ def tile_transformerblock_pb_kernel(tc, attn, x, w_out, b_out, ln2_g, ln2_b, w1,
     x_mid_rows = out_0.flatten_outer_dims().rearrange("(p i) d -> p i d", i=TOKEN_TILES)
     hid_rows = out_1.flatten_outer_dims().rearrange("(p i) f -> p i f", i=TOKEN_TILES)
     w_out_rows = w_out.rearrange("(g p t) n -> g p t n", g=PASSES, p=P, t=PACK)
-    w1_rows = w1.rearrange("(c b t i) f -> c t b i f", c=PASSES, t=PACK, i=RUN_K)
+    w1_rows = w1.rearrange("(c p t) f -> c p t f", c=PASSES, p=P, t=PACK)
 
     with ExitStack() as ctx:
         keep = ctx.enter_context(tc.tile_pool(name="keep", bufs=1))
@@ -80,32 +79,24 @@ def tile_transformerblock_pb_kernel(tc, attn, x, w_out, b_out, ln2_g, ln2_b, w1,
         def load_w1(load):
             half, c = divmod(load, PASSES)
             w1_raw[load] = raw.tile([P, PACK, HALF], BF16, name="w1_raw%d" % load, tag="raw")
-            for t in range(PACK):
-                nc.sync.dma_start(out=w1_raw[load][:, t, :], in_=w1_rows[c, t, :, :, HALF * half : HALF * (half + 1)])
+            nc.sync.dma_start(out=w1_raw[load][:], in_=w1_rows[c, :, :, HALF * half : HALF * (half + 1)])
 
         w_out_raw = raw_tile("w_out_raw")
         w_out_pieces = [(g, slice(PIECE * n, PIECE * (n + 1))) for g in range(PASSES) for n in range(WIDTH // PIECE)]
 
-        def load_w_out(piece):
-            g, cols = piece
-            nc.sync.dma_start(out=w_out_raw[:, PACK * g : PACK * (g + 1), cols], in_=w_out_rows[g, :, :, cols])
+        def load_w_out(g):
+            nc.sync.dma_start(out=w_out_raw[:, PACK * g : PACK * (g + 1), :], in_=w_out_rows[g])
 
-        load_w_out(w_out_pieces[0])
+        load_w_out(0)
         b_out_row = keep.tile([P, WIDTH], BF16, name="b_out_row")
         nc.vector.memset(b_out_row[:], 0.0)
         nc.sync.dma_start(out=b_out_row[0:1, :], in_=b_out.rearrange("(o d) -> o d", o=1))
 
-        gain_bias_rows = keep.tile([P, P], BF16, name="gain_bias_rows")
-        nc.vector.memset(gain_bias_rows[:], 0.0)
-        for v, vector in enumerate((ln2_g, ln2_b)):
-            vector_rows = vector.rearrange("(c b t i) -> c t b i", c=PASSES, t=PACK, i=RUN_K)
-            for c in range(PASSES):
-                first = K_ROWS * v + PACK * c
-                nc.sync.dma_start(
-                    out=gain_bias_rows[first : first + PACK, :].rearrange("t (b i) -> t b i", i=RUN_K), in_=vector_rows[c]
-                )
-        for piece in w_out_pieces[1:]:
-            load_w_out(piece)
+        gain_raw = keep.tile([P, PASSES, PACK], BF16, name="gain_raw")
+        bias_raw = keep.tile([P, PASSES, PACK], BF16, name="bias_raw")
+        nc.sync.dma_start(out=gain_raw[:], in_=ln2_g.rearrange("(c p t) -> p c t", c=PASSES, t=PACK))
+        nc.sync.dma_start(out=bias_raw[:], in_=ln2_b.rearrange("(c p t) -> p c t", c=PASSES, t=PACK))
+        load_w_out(1)
         attn_raw = raw_tile("attn_raw")
         x_raw = {}
         for q in range(PAIRS):
@@ -137,12 +128,8 @@ def tile_transformerblock_pb_kernel(tc, attn, x, w_out, b_out, ln2_g, ln2_b, w1,
             nc.scalar.copy(out=b_out_all[:, cols], in_=spread[:])
 
         gain_bias = keep.tile([P, 2 * K_ROWS], F32, name="gain_bias")
-
-        gain_bias_f32 = keep.tile([P, P], F32, name="gain_bias_f32")
-        nc.vector.tensor_copy(out=gain_bias_f32[:], in_=gain_bias_rows[:])
-        gain_bias_t = bank("gain_bias_t")
-        nc.tensor.transpose(out=gain_bias_t[:, 0:P], in_=gain_bias_f32[:], identity=identity[:])
-        nc.vector.tensor_copy(out=gain_bias[:], in_=gain_bias_t[:, 0 : 2 * K_ROWS])
+        nc.vector.tensor_copy(out=gain_bias[:, 0:K_ROWS], in_=gain_raw[:].rearrange("p c t -> p (c t)"))
+        nc.vector.tensor_copy(out=gain_bias[:, K_ROWS:], in_=bias_raw[:].rearrange("p c t -> p (c t)"))
 
         def quantised(name, outer, width):
             words = keep.tile([P, outer, width], U32, name=name + "_words", align_bytes=64)
@@ -283,24 +270,21 @@ def tile_transformerblock_pb_kernel(tc, attn, x, w_out, b_out, ln2_g, ln2_b, w1,
 
         def normalise(i):
             normed[i] = row("normed")
-            for c in range(PASSES):
-                cols = slice(K_PASS * c, K_PASS * (c + 1))
-                nc.vector.tensor_scalar(
-                    out=normed[i][:, cols].rearrange("n (t b i) -> n t b i", t=PACK, i=RUN_K),
-                    in0=x_mid[i][:, cols].rearrange("n (b t i) -> n t b i", t=PACK, i=RUN_K),
-                    scalar1=neg_mean[:, i : i + 1], scalar2=rstd[:, i : i + 1], op0=ALU.add, op1=ALU.mult,
-                )
+            nc.vector.tensor_scalar(
+                out=normed[i][:], in0=x_mid[i][:], scalar1=neg_mean[:, i : i + 1], scalar2=rstd[:, i : i + 1],
+                op0=ALU.add, op1=ALU.mult,
+            )
 
         def transpose_normed(q):
             h2_planes[q] = packs.tile([P, PACK, PASSES * PAIR_TOKENS], BF16, name="h2_planes")
             for half in range(K_ROWS // 2):
                 normed_t = bank("normed_t")
                 for s in range(2):
-                    r = 2 * half + s
+                    c, t = divmod(2 * half + s, PACK)
                     for m in range(PAIR):
                         nc.tensor.transpose(
                             out=normed_t[:, PAIR_TOKENS * s + P * m : PAIR_TOKENS * s + P * (m + 1)],
-                            in_=normed[PAIR * q + m][:, P * r : P * (r + 1)], identity=identity[:],
+                            in_=normed[PAIR * q + m][:, K_PASS * c + t : K_PASS * (c + 1) : PACK], identity=identity[:],
                         )
                 for s in range(2):
                     r = 2 * half + s

@@ -17,8 +17,10 @@ K_PASS = P * PACK
 BANK = 512
 RAW_BUFS = 3
 ROW_BUFS = 20
-C0_AFTER = 2
-VECTOR_BIAS_TILES = 4
+W_OUT_SPLIT = 320
+QUANTISE_LAG = 2
+TAIL = 256
+C0_AFTER = 1
 SCALAR_PIECES = (3, 5, 7, 9, 11, 13, 15)
 RUN = 4
 
@@ -84,10 +86,8 @@ def tile_transformerblock_pb_kernel(tc, attn, x, w_out, b_out, ln2_g, ln2_b, w1,
         w_out_raw = raw_tile("w_out_raw")
         w_out_pieces = [(g, slice(PIECE * n, PIECE * (n + 1))) for g in range(PASSES) for n in range(WIDTH // PIECE)]
 
-        def load_w_out(g):
-            nc.sync.dma_start(out=w_out_raw[:, PACK * g : PACK * (g + 1), :], in_=w_out_rows[g])
-
-        load_w_out(0)
+        for cols in (slice(0, PIECE), slice(PIECE, WIDTH)):
+            nc.sync.dma_start(out=w_out_raw[:, 0:PACK, cols], in_=w_out_rows[0, :, :, cols])
         b_out_row = keep.tile([P, WIDTH], BF16, name="b_out_row")
         nc.vector.memset(b_out_row[:], 0.0)
         nc.sync.dma_start(out=b_out_row[0:1, :], in_=b_out.rearrange("(o d) -> o d", o=1))
@@ -96,7 +96,7 @@ def tile_transformerblock_pb_kernel(tc, attn, x, w_out, b_out, ln2_g, ln2_b, w1,
         bias_raw = keep.tile([P, PASSES, PACK], BF16, name="bias_raw")
         nc.sync.dma_start(out=gain_raw[:], in_=ln2_g.rearrange("(c p t) -> p c t", c=PASSES, t=PACK))
         nc.sync.dma_start(out=bias_raw[:], in_=ln2_b.rearrange("(c p t) -> p c t", c=PASSES, t=PACK))
-        load_w_out(1)
+        nc.sync.dma_start(out=w_out_raw[:, PACK : 2 * PACK, :], in_=w_out_rows[1])
         attn_raw = raw_tile("attn_raw")
         x_raw = {}
         for q in range(PAIRS):
@@ -120,12 +120,6 @@ def tile_transformerblock_pb_kernel(tc, attn, x, w_out, b_out, ln2_g, ln2_b, w1,
         nc.vector.tensor_copy(out=identity_bf16[:], in_=identity[:])
         ones = keep.tile([P, P], BF16, name="ones")
         nc.vector.memset(ones[:], 1.0)
-        b_out_all = keep.tile([P, WIDTH], BF16, name="b_out_all")
-        for n in range(WIDTH // BANK):
-            cols = slice(BANK * n, BANK * (n + 1))
-            spread = bank("spread")
-            nc.tensor.matmul(out=spread[:], lhsT=ones[:], rhs=b_out_row[:, cols], start=True, stop=True)
-            nc.scalar.copy(out=b_out_all[:, cols], in_=spread[:])
 
         gain_bias = keep.tile([P, 2 * K_ROWS], F32, name="gain_bias")
         nc.vector.tensor_copy(out=gain_bias[:, 0:K_ROWS], in_=gain_raw[:].rearrange("p c t -> p (c t)"))
@@ -155,9 +149,12 @@ def tile_transformerblock_pb_kernel(tc, attn, x, w_out, b_out, ln2_g, ln2_b, w1,
 
         piece_tiles = {}
 
-        def regroup_piece(key, copy, raw_rows):
+        def new_piece(key):
             piece_tiles[key] = rows.tile([P, PACK * PIECE], BF16, name="piece", tag="row", align_bytes=64)
-            regroup(copy, piece_tiles[key][:], raw_rows)
+            return piece_tiles[key]
+
+        def regroup_piece(key, copy, raw_rows):
+            regroup(copy, new_piece(key)[:], raw_rows)
 
         def w1_piece(k):
             load, n = divmod(k, HALF // PIECE)
@@ -170,15 +167,19 @@ def tile_transformerblock_pb_kernel(tc, attn, x, w_out, b_out, ln2_g, ln2_b, w1,
                 load, c, cols, cols_in_load = w1_piece(k)
                 copy = nc.scalar.copy if k in SCALAR_PIECES else nc.vector.tensor_copy
                 regroup_piece(("w1", k), copy, w1_raw[load][:, :, cols_in_load])
-            if 1 <= k <= W1_PIECES:
-                load, c, cols, cols_in_load = w1_piece(k - 1)
-                quantise(piece_tiles[("w1", k - 1)][:], w1_words[:, c, cols], w1_scales[:, c, cols])
+            if k >= QUANTISE_LAG:
+                load, c, cols, cols_in_load = w1_piece(k - QUANTISE_LAG)
+                quantise(piece_tiles[("w1", k - QUANTISE_LAG)][:], w1_words[:, c, cols], w1_scales[:, c, cols])
 
         for k in range(len(w_out_pieces) + 1):
             if k < len(w_out_pieces):
                 g, cols = w_out_pieces[k]
-                copy = nc.vector.tensor_copy if k % 2 == 0 else nc.scalar.copy
-                regroup_piece(("w_out", k), copy, w_out_raw[:, PACK * g : PACK * (g + 1), cols])
+                piece = new_piece(("w_out", k))
+                for copy, share in ((nc.vector.tensor_copy, slice(0, W_OUT_SPLIT)), (nc.scalar.copy, slice(W_OUT_SPLIT, PIECE))):
+                    regroup(
+                        copy, piece[:, PACK * share.start : PACK * share.stop],
+                        w_out_raw[:, PACK * g : PACK * (g + 1), cols.start + share.start : cols.start + share.stop],
+                    )
             if k > 0:
                 g, cols = w_out_pieces[k - 1]
                 quantise(piece_tiles[("w_out", k - 1)][:], w_out_words[:, g, cols], w_out_scales[:, g, cols])
@@ -210,7 +211,6 @@ def tile_transformerblock_pb_kernel(tc, attn, x, w_out, b_out, ln2_g, ln2_b, w1,
         x_bias = {}
         x_mid = {}
         row_sums = keep.tile([P, TOKEN_TILES, WIDTH // BANK], F32, name="row_sums")
-        scaled_sums = keep.tile([P, WIDTH // BANK], F32, name="scaled_sums")
         neg_mean = keep.tile([P, TOKEN_TILES], F32, name="neg_mean")
         squares = keep.tile([P, WIDTH], BF16, name="squares")
         sum_sq = keep.tile([P, TOKEN_TILES], F32, name="sum_sq")
@@ -220,9 +220,6 @@ def tile_transformerblock_pb_kernel(tc, attn, x, w_out, b_out, ln2_g, ln2_b, w1,
         def add_b_out(i):
             x_tile = x_raw[i // PAIR][:, i % PAIR, :]
             x_bias[i] = row("x_bias")
-            if i < VECTOR_BIAS_TILES:
-                nc.vector.tensor_tensor(out=x_bias[i][:], in0=x_tile, in1=b_out_all[:], op=ALU.add)
-                return
             for n in range(WIDTH // BANK):
                 cols = slice(BANK * n, BANK * (n + 1))
                 sums = bank("x_bias_sums")
@@ -246,11 +243,13 @@ def tile_transformerblock_pb_kernel(tc, attn, x, w_out, b_out, ln2_g, ln2_b, w1,
                 )
             nc.sync.dma_start(out=x_mid_rows[:, i, :], in_=x_mid[i][:])
 
-        def row_statistics(i):
-            nc.scalar.activation(
-                out=scaled_sums[:], in_=row_sums[:, i, :], func=ACT.Identity, scale=-1.0 / WIDTH,
-                accum_out=neg_mean[:, i : i + 1],
+        def mean_of_rows(i):
+            nc.gpsimd.tensor_scalar(
+                out=neg_mean[:, i : i + 1], in0=row_sums[:, i, 0:1], scalar1=row_sums[:, i, 1:2], scalar2=-1.0 / WIDTH,
+                op0=ALU.add, op1=ALU.mult,
             )
+
+        def squares_of_rows(i):
             nc.scalar.activation(
                 out=squares[:], in_=x_mid[i][:], func=ACT.Square, bias=neg_mean[:, i : i + 1],
                 accum_out=sum_sq[:, i : i + 1],
@@ -304,6 +303,8 @@ def tile_transformerblock_pb_kernel(tc, attn, x, w_out, b_out, ln2_g, ln2_b, w1,
 
         hid = {}
 
+        hid_acc = {}
+
         def hid_multiply(j, i):
             q, m = divmod(i, PAIR)
 
@@ -311,13 +312,18 @@ def tile_transformerblock_pb_kernel(tc, attn, x, w_out, b_out, ln2_g, ln2_b, w1,
                 tokens = slice(PAIR_TOKENS * c + P * m, PAIR_TOKENS * c + P * (m + 1))
                 return h2_words[:, q, tokens], h2_scales[:, q, tokens]
 
-            hid[i] = row("hid")
             for n in range(CHUNK // BANK):
+                hid_acc[i, n] = bank("acc2")
                 cols = slice(CHUNK * j + BANK * n, CHUNK * j + BANK * (n + 1))
-                acc = bank("acc2")
-                multiply(acc[:], words_of_pass, w1_words, w1_scales, cols)
+                multiply(hid_acc[i, n][:], words_of_pass, w1_words, w1_scales, cols)
+
+        def hid_add(j, i, width):
+            hid[i] = row("hid")
+            for first in range(0, CHUNK, width):
+                n, within = divmod(first, BANK)
                 nc.vector.tensor_tensor(
-                    out=hid[i][:, BANK * n : BANK * (n + 1)], in0=acc[:], in1=b1_all[:, cols], op=ALU.add
+                    out=hid[i][:, first : first + width], in0=hid_acc[i, n][:, within : within + width],
+                    in1=b1_all[:, CHUNK * j + first : CHUNK * j + first + width], op=ALU.add,
                 )
 
         def hid_finish(j, i, width):
@@ -331,36 +337,40 @@ def tile_transformerblock_pb_kernel(tc, attn, x, w_out, b_out, ln2_g, ln2_b, w1,
         for i in range(PAIR):
             transpose_attn(i)
         for i in range(PAIR):
-            add_b_out(i)
             quantise_attn(i)
+            add_b_out(i)
         pieces_done = 0
-        for s in range(TOKEN_TILES * CHUNKS + 9):
+        for s in range(TOKEN_TILES * CHUNKS + 11):
             if s + PAIR < TOKEN_TILES:
                 transpose_attn(s + PAIR)
+            if s + PAIR < TOKEN_TILES:
                 add_b_out(s + PAIR)
             if s < TOKEN_TILES:
                 project(s)
+                mean_of_rows(s)
             if s + PAIR < TOKEN_TILES:
                 quantise_attn(s + PAIR)
             if 1 <= s < TOKEN_TILES + 1:
-                row_statistics(s - 1)
+                squares_of_rows(s - 1)
                 if s % PAIR == 0:
                     rstd_of_pair(s // PAIR - 1)
             if 4 <= s < TOKEN_TILES + 4:
                 normalise(s - 4)
             if (s - 4) % PAIR == 0 and 6 <= s < TOKEN_TILES + 6:
                 transpose_normed((s - 6) // PAIR)
-            if pieces_done <= W1_PIECES and s in (2, 3, 4, 5, 6, 7, 8, 9, 12, 14, 16, 18, 20, 22, 24, 26, 28):
+            if pieces_done < W1_PIECES + QUANTISE_LAG and s in (1, 2, 3, 4, 5, 6, 7, 8, 9, 10, 11, 12, 13, 14, 15, 16, 17, 18):
                 prepare_w1(pieces_done)
                 pieces_done += 1
-            if s in (6, 9):
+            if s in (6, 7):
                 load_w1(2 if s == 6 else 3)
             if (s - 7) % PAIR == 0 and 7 <= s < TOKEN_TILES + 7:
                 regroup_h2((s - 7) // PAIR)
             if (s - 8) % PAIR == 0 and 8 <= s < TOKEN_TILES + 8:
                 quantise_h2((s - 8) // PAIR)
-            if s >= 9:
+            if 9 <= s < TOKEN_TILES * CHUNKS + 9:
                 hid_multiply((s - 9) // TOKEN_TILES, (s - 9) % TOKEN_TILES)
-            if s >= 10:
-                hid_finish((s - 10) // TOKEN_TILES, (s - 10) % TOKEN_TILES, CHUNK)
-        hid_finish(CHUNKS - 1, TOKEN_TILES - 1, BANK)
+            if 10 <= s < TOKEN_TILES * CHUNKS + 10:
+                last = s == TOKEN_TILES * CHUNKS + 9
+                hid_add((s - 10) // TOKEN_TILES, (s - 10) % TOKEN_TILES, TAIL if last else BANK)
+            if s >= 11:
+                hid_finish((s - 11) // TOKEN_TILES, (s - 11) % TOKEN_TILES, TAIL if s == TOKEN_TILES * CHUNKS + 10 else CHUNK)

@@ -92,10 +92,6 @@ def tile_transformerblock_pb_kernel(tc, attn, x, w_out, b_out, ln2_g, ln2_b, w1,
         nc.vector.memset(b_out_row[:], 0.0)
         nc.sync.dma_start(out=b_out_row[0:1, :], in_=b_out.rearrange("(o d) -> o d", o=1))
 
-        gain_raw = keep.tile([P, PASSES, PACK], BF16, name="gain_raw")
-        bias_raw = keep.tile([P, PASSES, PACK], BF16, name="bias_raw")
-        nc.sync.dma_start(out=gain_raw[:], in_=ln2_g.rearrange("(c p t) -> p c t", c=PASSES, t=PACK))
-        nc.sync.dma_start(out=bias_raw[:], in_=ln2_b.rearrange("(c p t) -> p c t", c=PASSES, t=PACK))
         nc.sync.dma_start(out=w_out_raw[:, PACK : 2 * PACK, :], in_=w_out_rows[1])
         attn_raw = raw_tile("attn_raw")
         x_raw = {}
@@ -106,6 +102,10 @@ def tile_transformerblock_pb_kernel(tc, attn, x, w_out, b_out, ln2_g, ln2_b, w1,
             nc.sync.dma_start(out=x_raw[q][:], in_=x_rows[:, tiles, :])
             if q == C0_AFTER:
                 load_w1(0)
+                gain_raw = keep.tile([P, PASSES, PACK], BF16, name="gain_raw")
+                bias_raw = keep.tile([P, PASSES, PACK], BF16, name="bias_raw")
+                nc.sync.dma_start(out=gain_raw[:], in_=ln2_g.rearrange("(c p t) -> p c t", c=PASSES, t=PACK))
+                nc.sync.dma_start(out=bias_raw[:], in_=ln2_b.rearrange("(c p t) -> p c t", c=PASSES, t=PACK))
         load_w1(1)
         b1_all = keep.tile([P, HIDDEN], BF16, name="b1_all")
         nc.sync.dma_start(out=b1_all[:], in_=b1.partition_broadcast(P))
@@ -117,13 +117,15 @@ def tile_transformerblock_pb_kernel(tc, attn, x, w_out, b_out, ln2_g, ln2_b, w1,
         identity = keep.tile([P, P], F32, name="identity")
         masks.make_identity(nc, identity[:])
         identity_bf16 = keep.tile([P, P], BF16, name="identity_bf16")
-        nc.vector.tensor_copy(out=identity_bf16[:], in_=identity[:])
+        nc.gpsimd.tensor_copy(out=identity_bf16[:], in_=identity[:])
         ones = keep.tile([P, P], BF16, name="ones")
         nc.vector.memset(ones[:], 1.0)
 
         gain_bias = keep.tile([P, 2 * K_ROWS], F32, name="gain_bias")
-        nc.vector.tensor_copy(out=gain_bias[:, 0:K_ROWS], in_=gain_raw[:].rearrange("p c t -> p (c t)"))
-        nc.vector.tensor_copy(out=gain_bias[:, K_ROWS:], in_=bias_raw[:].rearrange("p c t -> p (c t)"))
+
+        def widen_gain_bias():
+            nc.vector.tensor_copy(out=gain_bias[:, 0:K_ROWS], in_=gain_raw[:].rearrange("p c t -> p (c t)"))
+            nc.vector.tensor_copy(out=gain_bias[:, K_ROWS:], in_=bias_raw[:].rearrange("p c t -> p (c t)"))
 
         def quantised(name, outer, width):
             words = keep.tile([P, outer, width], U32, name=name + "_words", align_bytes=64)
@@ -244,7 +246,7 @@ def tile_transformerblock_pb_kernel(tc, attn, x, w_out, b_out, ln2_g, ln2_b, w1,
             nc.sync.dma_start(out=x_mid_rows[:, i, :], in_=x_mid[i][:])
 
         def mean_of_rows(i):
-            nc.gpsimd.tensor_scalar(
+            nc.vector.tensor_scalar(
                 out=neg_mean[:, i : i + 1], in0=row_sums[:, i, 0:1], scalar1=row_sums[:, i, 1:2], scalar2=-1.0 / WIDTH,
                 op0=ALU.add, op1=ALU.mult,
             )
@@ -269,21 +271,24 @@ def tile_transformerblock_pb_kernel(tc, attn, x, w_out, b_out, ln2_g, ln2_b, w1,
 
         def normalise(i):
             normed[i] = row("normed")
-            nc.vector.tensor_scalar(
-                out=normed[i][:], in0=x_mid[i][:], scalar1=neg_mean[:, i : i + 1], scalar2=rstd[:, i : i + 1],
-                op0=ALU.add, op1=ALU.mult,
-            )
+            for c in range(PASSES):
+                cols = slice(K_PASS * c, K_PASS * (c + 1))
+                nc.vector.tensor_scalar(
+                    out=normed[i][:, cols].rearrange("p (t a i) -> p a t i", t=PACK, i=RUN),
+                    in0=x_mid[i][:, cols].rearrange("p (a i t) -> p a t i", t=PACK, i=RUN),
+                    scalar1=neg_mean[:, i : i + 1], scalar2=rstd[:, i : i + 1], op0=ALU.add, op1=ALU.mult,
+                )
 
         def transpose_normed(q):
             h2_planes[q] = packs.tile([P, PACK, PASSES * PAIR_TOKENS], BF16, name="h2_planes")
             for half in range(K_ROWS // 2):
                 normed_t = bank("normed_t")
                 for s in range(2):
-                    c, t = divmod(2 * half + s, PACK)
+                    r = 2 * half + s
                     for m in range(PAIR):
                         nc.tensor.transpose(
                             out=normed_t[:, PAIR_TOKENS * s + P * m : PAIR_TOKENS * s + P * (m + 1)],
-                            in_=normed[PAIR * q + m][:, K_PASS * c + t : K_PASS * (c + 1) : PACK], identity=identity[:],
+                            in_=normed[PAIR * q + m][:, P * r : P * (r + 1)], identity=identity[:],
                         )
                 for s in range(2):
                     r = 2 * half + s
@@ -347,13 +352,16 @@ def tile_transformerblock_pb_kernel(tc, attn, x, w_out, b_out, ln2_g, ln2_b, w1,
                 add_b_out(s + PAIR)
             if s < TOKEN_TILES:
                 project(s)
-                mean_of_rows(s)
             if s + PAIR < TOKEN_TILES:
                 quantise_attn(s + PAIR)
+            if s < TOKEN_TILES:
+                mean_of_rows(s)
             if 1 <= s < TOKEN_TILES + 1:
                 squares_of_rows(s - 1)
                 if s % PAIR == 0:
                     rstd_of_pair(s // PAIR - 1)
+            if s == 2:
+                widen_gain_bias()
             if 4 <= s < TOKEN_TILES + 4:
                 normalise(s - 4)
             if (s - 4) % PAIR == 0 and 6 <= s < TOKEN_TILES + 6:

@@ -22,6 +22,12 @@ QUANTISE_LAG = 2
 TAIL = 256
 C0_AFTER = 1
 SCALAR_PIECES = (3, 5, 7, 9, 11, 13, 15)
+TENSOR_PIECES = ()
+LATE = (10, 11, 14, 15)
+EARLY = [k for k in range(16) if k not in LATE]
+LATE_COLS = 512
+LATE_AT = 15
+LATE_QUANT = (29, 30, 31, 32)
 RUN = 4
 
 TOKENS = 1024
@@ -164,14 +170,53 @@ def tile_transformerblock_pb_kernel(tc, attn, x, w_out, b_out, ln2_g, ln2_b, w1,
             first = HALF * half + PIECE * n
             return load, c, slice(first, first + PIECE), slice(PIECE * n, PIECE * (n + 1))
 
-        def prepare_w1(k):
-            if k < W1_PIECES:
+        def prepare_w1(n):
+            if n < len(EARLY):
+                k = EARLY[n]
                 load, c, cols, cols_in_load = w1_piece(k)
-                copy = nc.scalar.copy if k in SCALAR_PIECES else nc.vector.tensor_copy
-                regroup_piece(("w1", k), copy, w1_raw[load][:, :, cols_in_load])
-            if k >= QUANTISE_LAG:
-                load, c, cols, cols_in_load = w1_piece(k - QUANTISE_LAG)
-                quantise(piece_tiles[("w1", k - QUANTISE_LAG)][:], w1_words[:, c, cols], w1_scales[:, c, cols])
+                raw_rows = w1_raw[load][:, :, cols_in_load]
+                if k in TENSOR_PIECES:
+                    regroup_on_tensor(("w1", k), raw_rows)
+                else:
+                    copy = nc.scalar.copy if k in SCALAR_PIECES else nc.vector.tensor_copy
+                    regroup_piece(("w1", k), copy, raw_rows)
+            if n >= QUANTISE_LAG:
+                quantise_w1(EARLY[n - QUANTISE_LAG])
+
+        def quantise_w1(k):
+            load, c, cols, cols_in_load = w1_piece(k)
+            quantise(piece_tiles[("w1", k)][:], w1_words[:, c, cols], w1_scales[:, c, cols])
+
+        def regroup_on_tensor(key, raw_rows):
+            piece = new_piece(key)
+            for half in range(2):
+                moved = psum.tile([P, 2 * BANK], BF16, name="moved", tag="bank")
+                for m in range(2):
+                    first = 2 * P * half + P * m
+                    nc.tensor.matmul(
+                        out=moved[:, BANK * m : BANK * (m + 1)], lhsT=identity_bf16[:],
+                        rhs=raw_rows[:, :, first : first + P].rearrange("p t w -> p w t"), start=True, stop=True,
+                    )
+                nc.scalar.copy(out=piece[:, 2 * BANK * half : 2 * BANK * (half + 1)], in_=moved[:])
+
+        late_go = keep.tile([P, 1], F32, name="late_go")
+        late_tile = {}
+
+        def regroup_late():
+            nc.vector.memset(late_go[:], 1.0)
+            late_tile[0] = raw_tile("late_grouped")
+            flat = late_tile[0][:].rearrange("p a b -> p (a b)")
+            for n, k in enumerate(LATE):
+                load, c, cols, cols_in_load = w1_piece(k)
+                piece_tiles[("w1", k)] = flat[:, PACK * PIECE * n : PACK * PIECE * (n + 1)]
+                for first in range(0, PIECE, LATE_COLS):
+                    grouped = piece_tiles[("w1", k)][:, PACK * first : PACK * (first + LATE_COLS)]
+                    raw_rows = w1_raw[load][:, :, cols_in_load.start + first : cols_in_load.start + first + LATE_COLS]
+                    nc.gpsimd.tensor_scalar(
+                        out=grouped.rearrange("p (a i t) -> p a t i", i=RUN, t=PACK),
+                        in0=raw_rows.rearrange("p t (a i) -> p a t i", i=RUN),
+                        scalar1=late_go[:], scalar2=0.0, op0=ALU.mult, op1=ALU.add,
+                    )
 
         for k in range(len(w_out_pieces) + 1):
             if k < len(w_out_pieces):
@@ -366,7 +411,11 @@ def tile_transformerblock_pb_kernel(tc, attn, x, w_out, b_out, ln2_g, ln2_b, w1,
                 normalise(s - 4)
             if (s - 4) % PAIR == 0 and 6 <= s < TOKEN_TILES + 6:
                 transpose_normed((s - 6) // PAIR)
-            if pieces_done < W1_PIECES + QUANTISE_LAG and s in (1, 2, 3, 4, 5, 6, 7, 8, 9, 10, 11, 12, 13, 14, 15, 16, 17, 18):
+            if s == LATE_AT and LATE:
+                regroup_late()
+            if LATE and s in LATE_QUANT:
+                quantise_w1(LATE[LATE_QUANT.index(s)])
+            if pieces_done < len(EARLY) + QUANTISE_LAG and 1 <= s:
                 prepare_w1(pieces_done)
                 pieces_done += 1
             if s in (6, 7):

@@ -16,18 +16,36 @@ PACK = 4
 K_PASS = P * PACK
 BANK = 512
 RAW_BUFS = 3
-ROW_BUFS = 20
+ROW_BUFS = 16
+PIECE_BUFS = 4
 W_OUT_SPLIT = 320
+LOADS = "o:00 o:01 o:1 s:b_out a:0 x:0 a:1 x:1 w:0 s:gain a:2 x:2 a:3 x:3 w:1 s:b1"
+QA = 0
+TRP = 1
+FINE = 1
+FW = 512
+SQ_AT = 1
+NORM_AT = 4
+TR_AT = 6
+QH_AT = 8
+HID_AT = 9
+LOAD_AT = (0, 5)
+XB_V = (0, 1, 2)
+HEAD = "ooOoOoOO"
+def EARLY_AT(s):
+    return 'w' if s in (1, 2) else 'wW' if s >= 3 else ''
+W_OUT_TENSOR = False
 QUANTISE_LAG = 2
 TAIL = 256
 C0_AFTER = 1
-SCALAR_PIECES = (3, 5, 7, 9, 11, 13, 15)
+SCALAR_PIECES = (3, 7, 8, 9, 13)
 TENSOR_PIECES = ()
 LATE = (10, 11, 14, 15)
 EARLY = [k for k in range(16) if k not in LATE]
 LATE_COLS = 512
 LATE_AT = 15
 LATE_QUANT = (29, 30, 31, 32)
+LATE_RG = (15, 16, 17, 18)
 RUN = 4
 
 TOKENS = 1024
@@ -72,6 +90,7 @@ def tile_transformerblock_pb_kernel(tc, attn, x, w_out, b_out, ln2_g, ln2_b, w1,
         attn_packs = ctx.enter_context(tc.tile_pool(name="attn_packs", bufs=3))
         packs = ctx.enter_context(tc.tile_pool(name="packs", bufs=2))
         rows = ctx.enter_context(tc.tile_pool(name="rows", bufs=ROW_BUFS))
+        pieces = ctx.enter_context(tc.tile_pool(name="pieces", bufs=PIECE_BUFS))
         psum = ctx.enter_context(tc.psum_pool(name="psum", bufs=8))
 
         ctx.enter_context(tc.manual_schedule())
@@ -91,30 +110,56 @@ def tile_transformerblock_pb_kernel(tc, attn, x, w_out, b_out, ln2_g, ln2_b, w1,
 
         w_out_raw = raw_tile("w_out_raw")
         w_out_pieces = [(g, slice(PIECE * n, PIECE * (n + 1))) for g in range(PASSES) for n in range(WIDTH // PIECE)]
-
-        for cols in (slice(0, PIECE), slice(PIECE, WIDTH)):
-            nc.sync.dma_start(out=w_out_raw[:, 0:PACK, cols], in_=w_out_rows[0, :, :, cols])
+        attn_raw = {}
+        x_raw = {}
         b_out_row = keep.tile([P, WIDTH], BF16, name="b_out_row")
         nc.vector.memset(b_out_row[:], 0.0)
-        nc.sync.dma_start(out=b_out_row[0:1, :], in_=b_out.rearrange("(o d) -> o d", o=1))
+        gain_raw = keep.tile([P, PASSES, PACK], BF16, name="gain_raw")
+        bias_raw = keep.tile([P, PASSES, PACK], BF16, name="bias_raw")
+        b1_all = keep.tile([P, HIDDEN], BF16, name="b1_all")
 
-        nc.sync.dma_start(out=w_out_raw[:, PACK : 2 * PACK, :], in_=w_out_rows[1])
-        attn_raw = raw_tile("attn_raw")
-        x_raw = {}
-        for q in range(PAIRS):
+        def load_w_out(g, cols):
+            nc.sync.dma_start(out=w_out_raw[:, PACK * g : PACK * (g + 1), cols], in_=w_out_rows[g, :, :, cols])
+
+        def load_w1_part(load, cols):
+            half, c = divmod(load, PASSES)
+            if load not in w1_raw:
+                w1_raw[load] = raw.tile([P, PACK, HALF], BF16, name="w1_raw%d" % load, tag="raw")
+            nc.sync.dma_start(
+                out=w1_raw[load][:, :, cols], in_=w1_rows[c, :, :, HALF * half + cols.start : HALF * half + cols.stop]
+            )
+
+        def load_attn(q):
             tiles = slice(PAIR * q, PAIR * (q + 1))
-            nc.sync.dma_start(out=attn_raw[:, tiles, :], in_=attn_rows[:, tiles, :])
+            attn_raw[q] = rows.tile([P, PAIR, WIDTH], BF16, name="attn_raw", tag="row", align_bytes=64)
+            nc.sync.dma_start(out=attn_raw[q][:], in_=attn_rows[:, tiles, :])
+
+        def load_x(q):
+            tiles = slice(PAIR * q, PAIR * (q + 1))
             x_raw[q] = rows.tile([P, PAIR, WIDTH], BF16, name="x_raw", tag="row", align_bytes=64)
             nc.sync.dma_start(out=x_raw[q][:], in_=x_rows[:, tiles, :])
-            if q == C0_AFTER:
-                load_w1(0)
-                gain_raw = keep.tile([P, PASSES, PACK], BF16, name="gain_raw")
-                bias_raw = keep.tile([P, PASSES, PACK], BF16, name="bias_raw")
+
+        def load_small(what):
+            if what == "b_out":
+                nc.sync.dma_start(out=b_out_row[0:1, :], in_=b_out.rearrange("(o d) -> o d", o=1))
+            if what == "gain":
                 nc.sync.dma_start(out=gain_raw[:], in_=ln2_g.rearrange("(c p t) -> p c t", c=PASSES, t=PACK))
                 nc.sync.dma_start(out=bias_raw[:], in_=ln2_b.rearrange("(c p t) -> p c t", c=PASSES, t=PACK))
-        load_w1(1)
-        b1_all = keep.tile([P, HIDDEN], BF16, name="b1_all")
-        nc.sync.dma_start(out=b1_all[:], in_=b1.partition_broadcast(P))
+            if what == "b1":
+                nc.sync.dma_start(out=b1_all[:], in_=b1.partition_broadcast(P))
+
+        for step in LOADS.split():
+            kind, n = step.split(":")
+            if kind == "o":
+                load_w_out(int(n[0]), slice(0, WIDTH) if len(n) == 1 else slice(PIECE * int(n[1]), PIECE * int(n[1]) + PIECE))
+            if kind == "w":
+                load_w1_part(int(n[0]), slice(0, HALF) if len(n) == 1 else slice(CHUNK * int(n[1]), CHUNK * int(n[1]) + CHUNK))
+            if kind == "a":
+                load_attn(int(n))
+            if kind == "x":
+                load_x(int(n))
+            if kind == "s":
+                load_small(n)
 
         neg_half = keep.tile([P, PAIR], F32, name="neg_half")
         nc.vector.memset(neg_half[:], -0.5)
@@ -158,7 +203,7 @@ def tile_transformerblock_pb_kernel(tc, attn, x, w_out, b_out, ln2_g, ln2_b, w1,
         piece_tiles = {}
 
         def new_piece(key):
-            piece_tiles[key] = rows.tile([P, PACK * PIECE], BF16, name="piece", tag="row", align_bytes=64)
+            piece_tiles[key] = pieces.tile([P, PACK * PIECE], BF16, name="piece", align_bytes=64)
             return piece_tiles[key]
 
         def regroup_piece(key, copy, raw_rows):
@@ -170,18 +215,14 @@ def tile_transformerblock_pb_kernel(tc, attn, x, w_out, b_out, ln2_g, ln2_b, w1,
             first = HALF * half + PIECE * n
             return load, c, slice(first, first + PIECE), slice(PIECE * n, PIECE * (n + 1))
 
-        def prepare_w1(n):
-            if n < len(EARLY):
-                k = EARLY[n]
-                load, c, cols, cols_in_load = w1_piece(k)
-                raw_rows = w1_raw[load][:, :, cols_in_load]
-                if k in TENSOR_PIECES:
-                    regroup_on_tensor(("w1", k), raw_rows)
-                else:
-                    copy = nc.scalar.copy if k in SCALAR_PIECES else nc.vector.tensor_copy
-                    regroup_piece(("w1", k), copy, raw_rows)
-            if n >= QUANTISE_LAG:
-                quantise_w1(EARLY[n - QUANTISE_LAG])
+        def regroup_w1(k):
+            load, c, cols, cols_in_load = w1_piece(k)
+            raw_rows = w1_raw[load][:, :, cols_in_load]
+            if k in TENSOR_PIECES:
+                regroup_on_tensor(("w1", k), raw_rows)
+            else:
+                copy = nc.scalar.copy if k in SCALAR_PIECES else nc.vector.tensor_copy
+                regroup_piece(("w1", k), copy, raw_rows)
 
         def quantise_w1(k):
             load, c, cols, cols_in_load = w1_piece(k)
@@ -191,24 +232,21 @@ def tile_transformerblock_pb_kernel(tc, attn, x, w_out, b_out, ln2_g, ln2_b, w1,
             piece = new_piece(key)
             for half in range(2):
                 moved = psum.tile([P, 2 * BANK], BF16, name="moved", tag="bank")
-                for m in range(2):
-                    first = 2 * P * half + P * m
+                for t in range(PACK):
                     nc.tensor.matmul(
-                        out=moved[:, BANK * m : BANK * (m + 1)], lhsT=identity_bf16[:],
-                        rhs=raw_rows[:, :, first : first + P].rearrange("p t w -> p w t"), start=True, stop=True,
+                        out=moved[:, t : 2 * BANK : PACK], lhsT=identity_bf16[:],
+                        rhs=raw_rows[:, t, 2 * P * half : 2 * P * (half + 1)], start=True, stop=True,
                     )
                 nc.scalar.copy(out=piece[:, 2 * BANK * half : 2 * BANK * (half + 1)], in_=moved[:])
 
         late_go = keep.tile([P, 1], F32, name="late_go")
         late_tile = {}
 
-        def regroup_late():
-            nc.vector.memset(late_go[:], 1.0)
-            late_tile[0] = raw_tile("late_grouped")
-            flat = late_tile[0][:].rearrange("p a b -> p (a b)")
-            for n, k in enumerate(LATE):
+        def regroup_late(n):
+            if 1:
+                k = LATE[n]
                 load, c, cols, cols_in_load = w1_piece(k)
-                piece_tiles[("w1", k)] = flat[:, PACK * PIECE * n : PACK * PIECE * (n + 1)]
+                new_piece(("w1", k))
                 for first in range(0, PIECE, LATE_COLS):
                     grouped = piece_tiles[("w1", k)][:, PACK * first : PACK * (first + LATE_COLS)]
                     raw_rows = w1_raw[load][:, :, cols_in_load.start + first : cols_in_load.start + first + LATE_COLS]
@@ -218,23 +256,46 @@ def tile_transformerblock_pb_kernel(tc, attn, x, w_out, b_out, ln2_g, ln2_b, w1,
                         scalar1=late_go[:], scalar2=0.0, op0=ALU.mult, op1=ALU.add,
                     )
 
-        for k in range(len(w_out_pieces) + 1):
-            if k < len(w_out_pieces):
-                g, cols = w_out_pieces[k]
-                piece = new_piece(("w_out", k))
-                for copy, share in ((nc.vector.tensor_copy, slice(0, W_OUT_SPLIT)), (nc.scalar.copy, slice(W_OUT_SPLIT, PIECE))):
-                    regroup(
-                        copy, piece[:, PACK * share.start : PACK * share.stop],
-                        w_out_raw[:, PACK * g : PACK * (g + 1), cols.start + share.start : cols.start + share.stop],
-                    )
-            if k > 0:
-                g, cols = w_out_pieces[k - 1]
-                quantise(piece_tiles[("w_out", k - 1)][:], w_out_words[:, g, cols], w_out_scales[:, g, cols])
+        def regroup_w_out(k):
+            g, cols = w_out_pieces[k]
+            if W_OUT_TENSOR:
+                regroup_on_tensor(("w_out", k), w_out_raw[:, PACK * g : PACK * (g + 1), cols])
+                return
+            piece = new_piece(("w_out", k))
+            for copy, share in ((nc.vector.tensor_copy, slice(0, W_OUT_SPLIT)), (nc.scalar.copy, slice(W_OUT_SPLIT, PIECE))):
+                regroup(
+                    copy, piece[:, PACK * share.start : PACK * share.stop],
+                    w_out_raw[:, PACK * g : PACK * (g + 1), cols.start + share.start : cols.start + share.stop],
+                )
+
+        def quantise_w_out(k):
+            g, cols = w_out_pieces[k]
+            quantise(piece_tiles[("w_out", k)][:], w_out_words[:, g, cols], w_out_scales[:, g, cols])
+
+        done = {"o": 0, "w": 0, "O": 0, "W": 0}
+
+        def weights(todo):
+            for kind in todo:
+                n = done[kind]
+                if kind == "o":
+                    regroup_w_out(n)
+                if kind == "O":
+                    quantise_w_out(n)
+                if kind in "wW" and n >= len(EARLY):
+                    continue
+                if kind == "w":
+                    regroup_w1(EARLY[n])
+                if kind == "W":
+                    assert n < done["w"]
+                    quantise_w1(EARLY[n])
+                done[kind] += 1
+
+        weights(HEAD)
 
         attn_grouped = {}
 
         def transpose_attn(i):
-            attn_pairs = attn_raw[:, i, :].bitcast(F32)
+            attn_pairs = attn_raw[i // PAIR][:, i % PAIR, :].bitcast(F32)
             attn_t = bank("attn_t")
             for g in range(PASSES):
                 for u in range(2):
@@ -259,14 +320,27 @@ def tile_transformerblock_pb_kernel(tc, attn, x, w_out, b_out, ln2_g, ln2_b, w1,
         x_mid = {}
         row_sums = keep.tile([P, TOKEN_TILES, WIDTH // BANK], F32, name="row_sums")
         neg_mean = keep.tile([P, TOKEN_TILES], F32, name="neg_mean")
+        scaled_sums = keep.tile([P, TOKEN_TILES, WIDTH // BANK], F32, name="scaled_sums")
         squares = keep.tile([P, WIDTH], BF16, name="squares")
         sum_sq = keep.tile([P, TOKEN_TILES], F32, name="sum_sq")
         var_eps = keep.tile([P, TOKEN_TILES], F32, name="var_eps")
         rstd = keep.tile([P, TOKEN_TILES], F32, name="rstd")
 
+        b_out_all = keep.tile([P, WIDTH], BF16, name="b_out_all")
+
+        def spread_b_out():
+            for n in range(WIDTH // BANK):
+                cols = slice(BANK * n, BANK * (n + 1))
+                spread = bank("spread")
+                nc.tensor.matmul(out=spread[:], lhsT=ones[:], rhs=b_out_row[:, cols], start=True, stop=True)
+                nc.scalar.copy(out=b_out_all[:, cols], in_=spread[:])
+
         def add_b_out(i):
             x_tile = x_raw[i // PAIR][:, i % PAIR, :]
             x_bias[i] = row("x_bias")
+            if i in XB_V:
+                nc.vector.tensor_tensor(out=x_bias[i][:], in0=x_tile, in1=b_out_all[:], op=ALU.add)
+                return
             for n in range(WIDTH // BANK):
                 cols = slice(BANK * n, BANK * (n + 1))
                 sums = bank("x_bias_sums")
@@ -291,9 +365,9 @@ def tile_transformerblock_pb_kernel(tc, attn, x, w_out, b_out, ln2_g, ln2_b, w1,
             nc.sync.dma_start(out=x_mid_rows[:, i, :], in_=x_mid[i][:])
 
         def mean_of_rows(i):
-            nc.vector.tensor_scalar(
-                out=neg_mean[:, i : i + 1], in0=row_sums[:, i, 0:1], scalar1=row_sums[:, i, 1:2], scalar2=-1.0 / WIDTH,
-                op0=ALU.add, op1=ALU.mult,
+            nc.scalar.activation(
+                out=scaled_sums[:, i, :], in_=row_sums[:, i, :], func=ACT.Copy, scale=-1.0 / WIDTH,
+                accum_out=neg_mean[:, i : i + 1],
             )
 
         def squares_of_rows(i):
@@ -316,24 +390,22 @@ def tile_transformerblock_pb_kernel(tc, attn, x, w_out, b_out, ln2_g, ln2_b, w1,
 
         def normalise(i):
             normed[i] = row("normed")
-            for c in range(PASSES):
-                cols = slice(K_PASS * c, K_PASS * (c + 1))
-                nc.vector.tensor_scalar(
-                    out=normed[i][:, cols].rearrange("p (t a i) -> p a t i", t=PACK, i=RUN),
-                    in0=x_mid[i][:, cols].rearrange("p (a i t) -> p a t i", t=PACK, i=RUN),
-                    scalar1=neg_mean[:, i : i + 1], scalar2=rstd[:, i : i + 1], op0=ALU.add, op1=ALU.mult,
-                )
+            nc.vector.tensor_scalar(
+                out=normed[i][:].rearrange("p (t a i) -> p a t i", t=PACK, i=RUN),
+                in0=x_mid[i][:].rearrange("p (a i t) -> p a t i", t=PACK, i=RUN),
+                scalar1=neg_mean[:, i : i + 1], scalar2=rstd[:, i : i + 1], op0=ALU.add, op1=ALU.mult,
+            )
 
         def transpose_normed(q):
             h2_planes[q] = packs.tile([P, PACK, PASSES * PAIR_TOKENS], BF16, name="h2_planes")
             for half in range(K_ROWS // 2):
                 normed_t = bank("normed_t")
                 for s in range(2):
-                    r = 2 * half + s
+                    c, t = divmod(2 * half + s, PACK)
                     for m in range(PAIR):
                         nc.tensor.transpose(
                             out=normed_t[:, PAIR_TOKENS * s + P * m : PAIR_TOKENS * s + P * (m + 1)],
-                            in_=normed[PAIR * q + m][:, P * r : P * (r + 1)], identity=identity[:],
+                            in_=normed[PAIR * q + m][:, PASSES * P * t + P * c : PASSES * P * t + P * (c + 1)], identity=identity[:],
                         )
                 for s in range(2):
                     r = 2 * half + s
@@ -384,50 +456,56 @@ def tile_transformerblock_pb_kernel(tc, attn, x, w_out, b_out, ln2_g, ln2_b, w1,
                     out=hid_rows[:, i, CHUNK * j + first : CHUNK * j + first + width], in_=part
                 )
 
+        if XB_V:
+            spread_b_out()
         for i in range(PAIR):
             transpose_attn(i)
         for i in range(PAIR):
             quantise_attn(i)
             add_b_out(i)
-        pieces_done = 0
-        for s in range(TOKEN_TILES * CHUNKS + 11):
-            if s + PAIR < TOKEN_TILES:
-                transpose_attn(s + PAIR)
-            if s + PAIR < TOKEN_TILES:
-                add_b_out(s + PAIR)
+        last_step = TOKEN_TILES * CHUNKS + HID_AT + 1
+        for s in range(last_step + 1):
             if s < TOKEN_TILES:
                 project(s)
             if s + PAIR < TOKEN_TILES:
+                if TRP and s % PAIR == 0:
+                    for i in range(PAIR):
+                        transpose_attn(s + PAIR + i)
+                if not TRP:
+                    transpose_attn(s + PAIR)
+                add_b_out(s + PAIR)
+            if s + PAIR < TOKEN_TILES and QA == 0:
                 quantise_attn(s + PAIR)
-            if s < TOKEN_TILES:
-                mean_of_rows(s)
-            if 1 <= s < TOKEN_TILES + 1:
-                squares_of_rows(s - 1)
-                if s % PAIR == 0:
-                    rstd_of_pair(s // PAIR - 1)
+            if SQ_AT <= s < TOKEN_TILES + SQ_AT:
+                mean_of_rows(s - SQ_AT)
+                squares_of_rows(s - SQ_AT)
+                if (s - SQ_AT) % PAIR == PAIR - 1:
+                    rstd_of_pair((s - SQ_AT) // PAIR)
             if s == 2:
                 widen_gain_bias()
-            if 4 <= s < TOKEN_TILES + 4:
-                normalise(s - 4)
-            if (s - 4) % PAIR == 0 and 6 <= s < TOKEN_TILES + 6:
-                transpose_normed((s - 6) // PAIR)
+            if NORM_AT <= s < TOKEN_TILES + NORM_AT:
+                normalise(s - NORM_AT)
+            if (s - TR_AT) % PAIR == 0 and TR_AT <= s < TOKEN_TILES + TR_AT:
+                transpose_normed((s - TR_AT) // PAIR)
             if s == LATE_AT and LATE:
-                regroup_late()
+                nc.vector.memset(late_go[:], 1.0)
             if LATE and s in LATE_QUANT:
                 quantise_w1(LATE[LATE_QUANT.index(s)])
-            if pieces_done < len(EARLY) + QUANTISE_LAG and 1 <= s:
-                prepare_w1(pieces_done)
-                pieces_done += 1
-            if s in (6, 7):
-                load_w1(2 if s == 6 else 3)
-            if (s - 7) % PAIR == 0 and 7 <= s < TOKEN_TILES + 7:
-                regroup_h2((s - 7) // PAIR)
-            if (s - 8) % PAIR == 0 and 8 <= s < TOKEN_TILES + 8:
-                quantise_h2((s - 8) // PAIR)
-            if 9 <= s < TOKEN_TILES * CHUNKS + 9:
-                hid_multiply((s - 9) // TOKEN_TILES, (s - 9) % TOKEN_TILES)
-            if 10 <= s < TOKEN_TILES * CHUNKS + 10:
-                last = s == TOKEN_TILES * CHUNKS + 9
-                hid_add((s - 10) // TOKEN_TILES, (s - 10) % TOKEN_TILES, TAIL if last else BANK)
-            if s >= 11:
-                hid_finish((s - 11) // TOKEN_TILES, (s - 11) % TOKEN_TILES, TAIL if s == TOKEN_TILES * CHUNKS + 10 else CHUNK)
+            if LATE and s in LATE_RG:
+                regroup_late(LATE_RG.index(s))
+            weights(EARLY_AT(s))
+            if s + PAIR < TOKEN_TILES and QA == 1:
+                quantise_attn(s + PAIR)
+            if s in LOAD_AT:
+                load_w1(2 + LOAD_AT.index(s))
+            if (s - TR_AT - 1) % PAIR == 0 and TR_AT + 1 <= s < TOKEN_TILES + TR_AT + 1:
+                regroup_h2((s - TR_AT - 1) // PAIR)
+            if (s - QH_AT) % PAIR == 0 and QH_AT <= s < TOKEN_TILES + QH_AT:
+                quantise_h2((s - QH_AT) // PAIR)
+            if HID_AT <= s < TOKEN_TILES * CHUNKS + HID_AT:
+                hid_multiply((s - HID_AT) // TOKEN_TILES, (s - HID_AT) % TOKEN_TILES)
+            if HID_AT + 1 <= s < TOKEN_TILES * CHUNKS + HID_AT + 1:
+                last = s == TOKEN_TILES * CHUNKS + HID_AT
+                hid_add((s - HID_AT - 1) // TOKEN_TILES, (s - HID_AT - 1) % TOKEN_TILES, TAIL if last else BANK)
+            if s >= HID_AT + 2:
+                hid_finish((s - HID_AT - 2) // TOKEN_TILES, (s - HID_AT - 2) % TOKEN_TILES, TAIL if s == last_step else FW if s >= last_step - FINE else CHUNK)

@@ -30,7 +30,7 @@ TR_AT = 6
 QH_AT = 8
 HID_AT = 9
 LOAD_AT = (0, 5)
-XB_V = (0, 1, 2)
+XB_V = (0, 2)
 HEAD = "ooOoOoOO"
 def EARLY_AT(s):
     return 'w' if s in (1, 2) else 'wW' if s >= 3 else ''
@@ -38,8 +38,8 @@ W_OUT_TENSOR = False
 QUANTISE_LAG = 2
 TAIL = 256
 C0_AFTER = 1
-SCALAR_PIECES = (3, 7, 8, 9, 13)
-TENSOR_PIECES = ()
+SCALAR_PIECES = (9, 13)
+TENSOR_PIECES = (3, 5, 6, 8, 12)
 LATE = (10, 11, 14, 15)
 EARLY = [k for k in range(16) if k not in LATE]
 LATE_COLS = 512
@@ -232,10 +232,13 @@ def tile_transformerblock_pb_kernel(tc, attn, x, w_out, b_out, ln2_g, ln2_b, w1,
             piece = new_piece(key)
             for half in range(2):
                 moved = psum.tile([P, 2 * BANK], BF16, name="moved", tag="bank")
-                for t in range(PACK):
+                for m in range(2):
+                    first = 2 * P * half + P * m
                     nc.tensor.matmul(
-                        out=moved[:, t : 2 * BANK : PACK], lhsT=identity_bf16[:],
-                        rhs=raw_rows[:, t, 2 * P * half : 2 * P * (half + 1)], start=True, stop=True,
+                        out=moved[:, BANK * m : BANK * (m + 1)].rearrange("p (a i t) -> p a t i", i=RUN, t=PACK),
+                        lhsT=identity_bf16[:],
+                        rhs=raw_rows[:, :, first : first + P].rearrange("p t (a i) -> p a t i", i=RUN),
+                        start=True, stop=True,
                     )
                 nc.scalar.copy(out=piece[:, 2 * BANK * half : 2 * BANK * (half + 1)], in_=moved[:])
 

from contextlib import ExitStack

import concourse.masks as masks
import concourse.mybir as mybir

F32 = mybir.dt.float32
BF16 = mybir.dt.bfloat16
U32 = mybir.dt.uint32
U8 = mybir.dt.uint8
FP8X4 = mybir.dt.float8_e4m3fn_x4
ALU = mybir.AluOpType
ACT = mybir.ActivationFunctionType

P = 128
PACK = 4
K_PASS = P * PACK
BANK = 512
RAW_BUFS = 3
ROW_BUFS = 16
PIECE_BUFS = 4
W_OUT_SPLIT = 320
LOADS = "o:00 o:01 o:1 s:b_out a:0 x:0 a:1 x:1 w:0 s:gain a:2 x:2 a:3 x:3 w:1 s:b1"
QA = 0
TRP = 1
FINE = 1
FW = 512
SQ_AT = 1
NORM_AT = 4
TR_AT = 6
QH_AT = 8
HID_AT = 9
LOAD_AT = (0, 5)
XB_V = (0, 2)
HEAD = "ooOoOoOO"
def EARLY_AT(s):
    return 'w' if s in (1, 2) else 'wW' if s >= 3 else ''
W_OUT_TENSOR = False
QUANTISE_LAG = 2
TAIL = 256
C0_AFTER = 1
SCALAR_PIECES = (9, 13)
TENSOR_PIECES = (3, 5, 6, 8, 12)
LATE = (10, 11, 14, 15)
EARLY = [k for k in range(16) if k not in LATE]
LATE_COLS = 512
LATE_AT = 15
LATE_QUANT = (29, 30, 31, 32)
LATE_RG = (15, 16, 17, 18)
RUN = 4

TOKENS = 1024
WIDTH = 1024
HIDDEN = 4096
EPS = 1e-5
TOKEN_TILES = TOKENS // P
K_ROWS = WIDTH // P
PASSES = WIDTH // K_PASS
CHUNK = 1024
CHUNKS = HIDDEN // CHUNK
HALF = HIDDEN // 2
PIECE = BANK
PIECES_PER_CHUNK = PASSES * (CHUNK // PIECE)
W1_PIECES = CHUNKS * PIECES_PER_CHUNK
PAIR = 2
PAIRS = TOKEN_TILES // PAIR
PAIR_TOKENS = PAIR * P

FLOPS = 2 * TOKENS * WIDTH * WIDTH + 2 * TOKENS * WIDTH * HIDDEN


def regroup(copy, grouped, rows):
    copy(
        out=grouped.rearrange("p (a i t) -> p a t i", i=RUN, t=PACK),
        in_=rows.rearrange("p t (a i) -> p a t i", i=RUN),
    )


def tile_transformerblock_pb_kernel(tc, attn, x, w_out, b_out, ln2_g, ln2_b, w1, b1, out_0, out_1):
    nc = tc.nc
    attn_rows = attn.flatten_outer_dims().rearrange("(p i) k -> p i k", i=TOKEN_TILES)
    x_rows = x.flatten_outer_dims().rearrange("(p i) d -> p i d", i=TOKEN_TILES)
    x_mid_rows = out_0.flatten_outer_dims().rearrange("(p i) d -> p i d", i=TOKEN_TILES)
    hid_rows = out_1.flatten_outer_dims().rearrange("(p i) f -> p i f", i=TOKEN_TILES)
    w_out_rows = w_out.rearrange("(g p t) n -> g p t n", g=PASSES, p=P, t=PACK)
    w1_rows = w1.rearrange("(c p t) f -> c p t f", c=PASSES, p=P, t=PACK)

    with ExitStack() as ctx:
        keep = ctx.enter_context(tc.tile_pool(name="keep", bufs=1))
        raw = ctx.enter_context(tc.tile_pool(name="raw", bufs=RAW_BUFS))
        attn_packs = ctx.enter_context(tc.tile_pool(name="attn_packs", bufs=3))
        packs = ctx.enter_context(tc.tile_pool(name="packs", bufs=2))
        rows = ctx.enter_context(tc.tile_pool(name="rows", bufs=ROW_BUFS))
        pieces = ctx.enter_context(tc.tile_pool(name="pieces", bufs=PIECE_BUFS))
        psum = ctx.enter_context(tc.psum_pool(name="psum", bufs=8))

        ctx.enter_context(tc.manual_schedule())

        def bank(name):
            return psum.tile([P, BANK], F32, name=name, tag="bank")

        def raw_tile(name):
            return raw.tile([P, PASSES * PACK, CHUNK], BF16, name=name, tag="raw")

        w1_raw = {}

        def load_w1(load):
            half, c = divmod(load, PASSES)
            w1_raw[load] = raw.tile([P, PACK, HALF], BF16, name="w1_raw%d" % load, tag="raw")
            nc.sync.dma_start(out=w1_raw[load][:], in_=w1_rows[c, :, :, HALF * half : HALF * (half + 1)])

        w_out_raw = raw_tile("w_out_raw")
        w_out_pieces = [(g, slice(PIECE * n, PIECE * (n + 1))) for g in range(PASSES) for n in range(WIDTH // PIECE)]
        attn_raw = {}
        x_raw = {}
        b_out_row = keep.tile([P, WIDTH], BF16, name="b_out_row")
        nc.vector.memset(b_out_row[:], 0.0)
        gain_raw = keep.tile([P, PASSES, PACK], BF16, name="gain_raw")
        bias_raw = keep.tile([P, PASSES, PACK], BF16, name="bias_raw")
        b1_all = keep.tile([P, HIDDEN], BF16, name="b1_all")

        def load_w_out(g, cols):
            nc.sync.dma_start(out=w_out_raw[:, PACK * g : PACK * (g + 1), cols], in_=w_out_rows[g, :, :, cols])

        def load_w1_part(load, cols):
            half, c = divmod(load, PASSES)
            if load not in w1_raw:
                w1_raw[load] = raw.tile([P, PACK, HALF], BF16, name="w1_raw%d" % load, tag="raw")
            nc.sync.dma_start(
                out=w1_raw[load][:, :, cols], in_=w1_rows[c, :, :, HALF * half + cols.start : HALF * half + cols.stop]
            )

        def load_attn(q):
            tiles = slice(PAIR * q, PAIR * (q + 1))
            attn_raw[q] = rows.tile([P, PAIR, WIDTH], BF16, name="attn_raw", tag="row", align_bytes=64)
            nc.sync.dma_start(out=attn_raw[q][:], in_=attn_rows[:, tiles, :])

        def load_x(q):
            tiles = slice(PAIR * q, PAIR * (q + 1))
            x_raw[q] = rows.tile([P, PAIR, WIDTH], BF16, name="x_raw", tag="row", align_bytes=64)
            nc.sync.dma_start(out=x_raw[q][:], in_=x_rows[:, tiles, :])

        def load_small(what):
            if what == "b_out":
                nc.sync.dma_start(out=b_out_row[0:1, :], in_=b_out.rearrange("(o d) -> o d", o=1))
            if what == "gain":
                nc.sync.dma_start(out=gain_raw[:], in_=ln2_g.rearrange("(c p t) -> p c t", c=PASSES, t=PACK))
                nc.sync.dma_start(out=bias_raw[:], in_=ln2_b.rearrange("(c p t) -> p c t", c=PASSES, t=PACK))
            if what == "b1":
                nc.sync.dma_start(out=b1_all[:], in_=b1.partition_broadcast(P))

        for step in LOADS.split():
            kind, n = step.split(":")
            if kind == "o":
                load_w_out(int(n[0]), slice(0, WIDTH) if len(n) == 1 else slice(PIECE * int(n[1]), PIECE * int(n[1]) + PIECE))
            if kind == "w":
                load_w1_part(int(n[0]), slice(0, HALF) if len(n) == 1 else slice(CHUNK * int(n[1]), CHUNK * int(n[1]) + CHUNK))
            if kind == "a":
                load_attn(int(n))
            if kind == "x":
                load_x(int(n))
            if kind == "s":
                load_small(n)

        neg_half = keep.tile([P, PAIR], F32, name="neg_half")
        nc.vector.memset(neg_half[:], -0.5)
        table_warm = keep.tile([P, 1], F32, name="table_warm")
        nc.scalar.activation(out=table_warm[:], in_=neg_half[:, 0:1], func=ACT.Gelu)
        identity = keep.tile([P, P], F32, name="identity")
        masks.make_identity(nc, identity[:])
        identity_bf16 = keep.tile([P, P], BF16, name="identity_bf16")
        nc.gpsimd.tensor_copy(out=identity_bf16[:], in_=identity[:])
        ones = keep.tile([P, P], BF16, name="ones")
        nc.vector.memset(ones[:], 1.0)

        gain_bias = keep.tile([P, 2 * K_ROWS], F32, name="gain_bias")

        def widen_gain_bias():
            nc.vector.tensor_copy(out=gain_bias[:, 0:K_ROWS], in_=gain_raw[:].rearrange("p c t -> p (c t)"))
            nc.vector.tensor_copy(out=gain_bias[:, K_ROWS:], in_=bias_raw[:].rearrange("p c t -> p (c t)"))

        def quantised(name, outer, width):
            words = keep.tile([P, outer, width], U32, name=name + "_words", align_bytes=64)
            scales = keep.tile([P, outer, width], U8, name=name + "_scales", align_bytes=64)
            return words, scales

        w_out_words, w_out_scales = quantised("w_out", PASSES, WIDTH)
        w1_words, w1_scales = quantised("w1", PASSES, HIDDEN)
        attn_words, attn_scales = quantised("attn", TOKEN_TILES, PASSES * P)
        h2_words, h2_scales = quantised("h2", PAIRS, PASSES * PAIR_TOKENS)

        def quantise(grouped, words, scales):
            nc.vector.quantize_mx(out=words.bitcast(FP8X4), scales=scales, in_=grouped)

        def multiply(acc, words_of_pass, rhs_words, rhs_scales, cols):
            for c in range(PASSES):
                lhs_words, lhs_scales = words_of_pass(c)
                nc.tensor.matmul_mx(
                    out=acc, lhsT=lhs_words.bitcast(FP8X4), lhsT_scale=lhs_scales,
                    rhs=rhs_words[:, c, cols].bitcast(FP8X4), rhs_scale=rhs_scales[:, c, cols],
                    start=(c == 0), stop=(c == PASSES - 1),
                )

        piece_tiles = {}

        def new_piece(key):
            piece_tiles[key] = pieces.tile([P, PACK * PIECE], BF16, name="piece", align_bytes=64)
            return piece_tiles[key]

        def regroup_piece(key, copy, raw_rows):
            regroup(copy, new_piece(key)[:], raw_rows)

        def w1_piece(k):
            load, n = divmod(k, HALF // PIECE)
            half, c = divmod(load, PASSES)
            first = HALF * half + PIECE * n
            return load, c, slice(first, first + PIECE), slice(PIECE * n, PIECE * (n + 1))

        def regroup_w1(k):
            load, c, cols, cols_in_load = w1_piece(k)
            raw_rows = w1_raw[load][:, :, cols_in_load]
            if k in TENSOR_PIECES:
                regroup_on_tensor(("w1", k), raw_rows)
            else:
                copy = nc.scalar.copy if k in SCALAR_PIECES else nc.vector.tensor_copy
                regroup_piece(("w1", k), copy, raw_rows)

        def quantise_w1(k):
            load, c, cols, cols_in_load = w1_piece(k)
            quantise(piece_tiles[("w1", k)][:], w1_words[:, c, cols], w1_scales[:, c, cols])

        def regroup_on_tensor(key, raw_rows):
            piece = new_piece(key)
            for half in range(2):
                moved = psum.tile([P, 2 * BANK], BF16, name="moved", tag="bank")
                for m in range(2):
                    first = 2 * P * half + P * m
                    nc.tensor.matmul(
                        out=moved[:, BANK * m : BANK * (m + 1)].rearrange("p (a i t) -> p a t i", i=RUN, t=PACK),
                        lhsT=identity_bf16[:],
                        rhs=raw_rows[:, :, first : first + P].rearrange("p t (a i) -> p a t i", i=RUN),
                        start=True, stop=True,
                    )
                nc.scalar.copy(out=piece[:, 2 * BANK * half : 2 * BANK * (half + 1)], in_=moved[:])

        late_go = keep.tile([P, 1], F32, name="late_go")
        late_tile = {}

        def regroup_late(n):
            if 1:
                k = LATE[n]
                load, c, cols, cols_in_load = w1_piece(k)
                new_piece(("w1", k))
                for first in range(0, PIECE, LATE_COLS):
                    grouped = piece_tiles[("w1", k)][:, PACK * first : PACK * (first + LATE_COLS)]
                    raw_rows = w1_raw[load][:, :, cols_in_load.start + first : cols_in_load.start + first + LATE_COLS]
                    nc.gpsimd.tensor_scalar(
                        out=grouped.rearrange("p (a i t) -> p a t i", i=RUN, t=PACK),
                        in0=raw_rows.rearrange("p t (a i) -> p a t i", i=RUN),
                        scalar1=late_go[:], scalar2=0.0, op0=ALU.mult, op1=ALU.add,
                    )

        def regroup_w_out(k):
            g, cols = w_out_pieces[k]
            if W_OUT_TENSOR:
                regroup_on_tensor(("w_out", k), w_out_raw[:, PACK * g : PACK * (g + 1), cols])
                return
            piece = new_piece(("w_out", k))
            for copy, share in ((nc.vector.tensor_copy, slice(0, W_OUT_SPLIT)), (nc.scalar.copy, slice(W_OUT_SPLIT, PIECE))):
                regroup(
                    copy, piece[:, PACK * share.start : PACK * share.stop],
                    w_out_raw[:, PACK * g : PACK * (g + 1), cols.start + share.start : cols.start + share.stop],
                )

        def quantise_w_out(k):
            g, cols = w_out_pieces[k]
            quantise(piece_tiles[("w_out", k)][:], w_out_words[:, g, cols], w_out_scales[:, g, cols])

        done = {"o": 0, "w": 0, "O": 0, "W": 0}

        def weights(todo):
            for kind in todo:
                n = done[kind]
                if kind == "o":
                    regroup_w_out(n)
                if kind == "O":
                    quantise_w_out(n)
                if kind in "wW" and n >= len(EARLY):
                    continue
                if kind == "w":
                    regroup_w1(EARLY[n])
                if kind == "W":
                    assert n < done["w"]
                    quantise_w1(EARLY[n])
                done[kind] += 1

        weights(HEAD)

        attn_grouped = {}

        def transpose_attn(i):
            attn_pairs = attn_raw[i // PAIR][:, i % PAIR, :].bitcast(F32)
            attn_t = bank("attn_t")
            for g in range(PASSES):
                for u in range(2):
                    nc.tensor.transpose(
                        out=attn_t[:, PASSES * P * u + P * g : PASSES * P * u + P * (g + 1)],
                        in_=attn_pairs[:, 2 * P * g + u : 2 * P * (g + 1) : 2],
                        identity=identity[:],
                    )
            attn_grouped[i] = attn_packs.tile([P, PACK * PASSES * P], BF16, name="attn_grouped", align_bytes=64)
            nc.scalar.copy(
                out=attn_grouped[i][:].bitcast(F32).rearrange("q (m u) -> q m u", u=2),
                in_=attn_t[:].rearrange("q (u m) -> q m u", u=2),
            )

        def quantise_attn(i):
            quantise(attn_grouped[i][:], attn_words[:, i, :], attn_scales[:, i, :])

        def row(name):
            return rows.tile([P, WIDTH], F32, name=name, tag="row", align_bytes=64)

        x_bias = {}
        x_mid = {}
        row_sums = keep.tile([P, TOKEN_TILES, WIDTH // BANK], F32, name="row_sums")
        neg_mean = keep.tile([P, TOKEN_TILES], F32, name="neg_mean")
        scaled_sums = keep.tile([P, TOKEN_TILES, WIDTH // BANK], F32, name="scaled_sums")
        squares = keep.tile([P, WIDTH], BF16, name="squares")
        sum_sq = keep.tile([P, TOKEN_TILES], F32, name="sum_sq")
        var_eps = keep.tile([P, TOKEN_TILES], F32, name="var_eps")
        rstd = keep.tile([P, TOKEN_TILES], F32, name="rstd")

        b_out_all = keep.tile([P, WIDTH], BF16, name="b_out_all")

        def spread_b_out():
            for n in range(WIDTH // BANK):
                cols = slice(BANK * n, BANK * (n + 1))
                spread = bank("spread")
                nc.tensor.matmul(out=spread[:], lhsT=ones[:], rhs=b_out_row[:, cols], start=True, stop=True)
                nc.scalar.copy(out=b_out_all[:, cols], in_=spread[:])

        def add_b_out(i):
            x_tile = x_raw[i // PAIR][:, i % PAIR, :]
            x_bias[i] = row("x_bias")
            if i in XB_V:
                nc.vector.tensor_tensor(out=x_bias[i][:], in0=x_tile, in1=b_out_all[:], op=ALU.add)
                return
            for n in range(WIDTH // BANK):
                cols = slice(BANK * n, BANK * (n + 1))
                sums = bank("x_bias_sums")
                nc.tensor.matmul(out=sums[:], lhsT=identity_bf16[:], rhs=x_tile[:, cols], start=True, stop=False)
                nc.tensor.matmul(out=sums[:], lhsT=ones[:], rhs=b_out_row[:, cols], start=False, stop=True)
                nc.scalar.copy(out=x_bias[i][:, cols], in_=sums[:])

        def project(i):
            def words_of_pass(c):
                tokens = slice(P * c, P * (c + 1))
                return attn_words[:, i, tokens], attn_scales[:, i, tokens]

            x_mid[i] = row("x_mid")
            for n in range(WIDTH // BANK):
                cols = slice(BANK * n, BANK * (n + 1))
                acc = bank("acc1")
                multiply(acc[:], words_of_pass, w_out_words, w_out_scales, cols)
                nc.vector.scalar_tensor_tensor(
                    out=x_mid[i][:, cols], in0=acc[:], scalar=1.0, in1=x_bias[i][:, cols],
                    op0=ALU.mult, op1=ALU.add, accum_out=row_sums[:, i, n : n + 1],
                )
            nc.sync.dma_start(out=x_mid_rows[:, i, :], in_=x_mid[i][:])

        def mean_of_rows(i):
            nc.scalar.activation(
                out=scaled_sums[:, i, :], in_=row_sums[:, i, :], func=ACT.Copy, scale=-1.0 / WIDTH,
                accum_out=neg_mean[:, i : i + 1],
            )

        def squares_of_rows(i):
            nc.scalar.activation(
                out=squares[:], in_=x_mid[i][:], func=ACT.Square, bias=neg_mean[:, i : i + 1],
                accum_out=sum_sq[:, i : i + 1],
            )

        def rstd_of_pair(q):
            tiles = slice(PAIR * q, PAIR * (q + 1))
            nc.gpsimd.tensor_scalar(
                out=var_eps[:, tiles], in0=sum_sq[:, tiles], scalar1=1.0 / WIDTH, scalar2=EPS, op0=ALU.mult, op1=ALU.add
            )
            nc.gpsimd.tensor_tensor(out=rstd[:, tiles], in0=var_eps[:, tiles], in1=neg_half[:], op=ALU.pow)

        h2_planes = {}
        h2_grouped = {}

        normed = {}

        def normalise(i):
            normed[i] = row("normed")
            nc.vector.tensor_scalar(
                out=normed[i][:].rearrange("p (t a i) -> p a t i", t=PACK, i=RUN),
                in0=x_mid[i][:].rearrange("p (a i t) -> p a t i", t=PACK, i=RUN),
                scalar1=neg_mean[:, i : i + 1], scalar2=rstd[:, i : i + 1], op0=ALU.add, op1=ALU.mult,
            )

        def transpose_normed(q):
            h2_planes[q] = packs.tile([P, PACK, PASSES * PAIR_TOKENS], BF16, name="h2_planes")
            for half in range(K_ROWS // 2):
                normed_t = bank("normed_t")
                for s in range(2):
                    c, t = divmod(2 * half + s, PACK)
                    for m in range(PAIR):
                        nc.tensor.transpose(
                            out=normed_t[:, PAIR_TOKENS * s + P * m : PAIR_TOKENS * s + P * (m + 1)],
                            in_=normed[PAIR * q + m][:, PASSES * P * t + P * c : PASSES * P * t + P * (c + 1)], identity=identity[:],
                        )
                for s in range(2):
                    r = 2 * half + s
                    c, t = divmod(r, PACK)
                    nc.scalar.activation(
                        out=h2_planes[q][:, t, PAIR_TOKENS * c : PAIR_TOKENS * (c + 1)],
                        in_=normed_t[:, PAIR_TOKENS * s : PAIR_TOKENS * (s + 1)],
                        func=ACT.Identity, scale=gain_bias[:, r : r + 1], bias=gain_bias[:, K_ROWS + r : K_ROWS + r + 1],
                    )

        def regroup_h2(q):
            h2_grouped[q] = packs.tile([P, PACK * PASSES * PAIR_TOKENS], BF16, name="h2_grouped", align_bytes=64)
            regroup(nc.vector.tensor_copy, h2_grouped[q][:], h2_planes[q][:])

        def quantise_h2(q):
            quantise(h2_grouped[q][:], h2_words[:, q, :], h2_scales[:, q, :])

        hid = {}

        hid_acc = {}

        def hid_multiply(j, i):
            q, m = divmod(i, PAIR)

            def words_of_pass(c):
                tokens = slice(PAIR_TOKENS * c + P * m, PAIR_TOKENS * c + P * (m + 1))
                return h2_words[:, q, tokens], h2_scales[:, q, tokens]

            for n in range(CHUNK // BANK):
                hid_acc[i, n] = bank("acc2")
                cols = slice(CHUNK * j + BANK * n, CHUNK * j + BANK * (n + 1))
                multiply(hid_acc[i, n][:], words_of_pass, w1_words, w1_scales, cols)

        def hid_add(j, i, width):
            hid[i] = row("hid")
            for first in range(0, CHUNK, width):
                n, within = divmod(first, BANK)
                nc.vector.tensor_tensor(
                    out=hid[i][:, first : first + width], in0=hid_acc[i, n][:, within : within + width],
                    in1=b1_all[:, CHUNK * j + first : CHUNK * j + first + width], op=ALU.add,
                )

        def hid_finish(j, i, width):
            for first in range(0, CHUNK, width):
                part = hid[i][:, first : first + width]
                nc.scalar.activation(out=part, in_=part, func=ACT.Gelu)
                nc.sync.dma_start(
                    out=hid_rows[:, i, CHUNK * j + first : CHUNK * j + first + width], in_=part
                )

        if XB_V:
            spread_b_out()
        for i in range(PAIR):
            transpose_attn(i)
        for i in range(PAIR):
            quantise_attn(i)
            add_b_out(i)
        last_step = TOKEN_TILES * CHUNKS + HID_AT + 1
        for s in range(last_step + 1):
            if s < TOKEN_TILES:
                project(s)
            if s + PAIR < TOKEN_TILES:
                if TRP and s % PAIR == 0:
                    for i in range(PAIR):
                        transpose_attn(s + PAIR + i)
                if not TRP:
                    transpose_attn(s + PAIR)
                add_b_out(s + PAIR)
            if s + PAIR < TOKEN_TILES and QA == 0:
                quantise_attn(s + PAIR)
            if SQ_AT <= s < TOKEN_TILES + SQ_AT:
                mean_of_rows(s - SQ_AT)
                squares_of_rows(s - SQ_AT)
                if (s - SQ_AT) % PAIR == PAIR - 1:
                    rstd_of_pair((s - SQ_AT) // PAIR)
            if s == 2:
                widen_gain_bias()
            if NORM_AT <= s < TOKEN_TILES + NORM_AT:
                normalise(s - NORM_AT)
            if (s - TR_AT) % PAIR == 0 and TR_AT <= s < TOKEN_TILES + TR_AT:
                transpose_normed((s - TR_AT) // PAIR)
            if s == LATE_AT and LATE:
                nc.vector.memset(late_go[:], 1.0)
            if LATE and s in LATE_QUANT:
                quantise_w1(LATE[LATE_QUANT.index(s)])
            if LATE and s in LATE_RG:
                regroup_late(LATE_RG.index(s))
            weights(EARLY_AT(s))
            if s + PAIR < TOKEN_TILES and QA == 1:
                quantise_attn(s + PAIR)
            if s in LOAD_AT:
                load_w1(2 + LOAD_AT.index(s))
            if (s - TR_AT - 1) % PAIR == 0 and TR_AT + 1 <= s < TOKEN_TILES + TR_AT + 1:
                regroup_h2((s - TR_AT - 1) // PAIR)
            if (s - QH_AT) % PAIR == 0 and QH_AT <= s < TOKEN_TILES + QH_AT:
                quantise_h2((s - QH_AT) // PAIR)
            if HID_AT <= s < TOKEN_TILES * CHUNKS + HID_AT:
                hid_multiply((s - HID_AT) // TOKEN_TILES, (s - HID_AT) % TOKEN_TILES)
            if HID_AT + 1 <= s < TOKEN_TILES * CHUNKS + HID_AT + 1:
                last = s == TOKEN_TILES * CHUNKS + HID_AT
                hid_add((s - HID_AT - 1) // TOKEN_TILES, (s - HID_AT - 1) % TOKEN_TILES, TAIL if last else BANK)
            if s >= HID_AT + 2:
                hid_finish((s - HID_AT - 2) // TOKEN_TILES, (s - HID_AT - 2) % TOKEN_TILES, TAIL if s == last_step else FW if s >= last_step - FINE else CHUNK)
